import numpy as np
import ml_dtypes


def mxq(x, axis, fmt="e4m3"):
    dtype, down = {"e4m3": (ml_dtypes.float8_e4m3fn, 7), "e5m2": (ml_dtypes.float8_e5m2, 14)}[fmt]
    v = np.moveaxis(np.asarray(x, np.float32).astype(ml_dtypes.bfloat16).astype(np.float64), axis, -1)
    blocks = v.reshape(v.shape[:-1] + (-1, 32))
    amax = np.abs(blocks).max(-1, keepdims=True)
    byte = np.maximum(np.where(amax > 0, np.frexp(amax)[1] - 1 + 127, 0) - down, 1)
    scale = np.exp2(byte - 127.0)
    codes = (blocks / scale).astype(np.float32).astype(dtype).astype(np.float64)
    return np.moveaxis((codes * scale).reshape(v.shape), -1, axis)


WIDE = False


def mx_kscale(k):
    if not WIDE:
        return np.ones(k)
    levels = np.array([10, -10, 5, -5, 0])
    if k % 512:
        return np.exp2(np.random.permutation(np.resize(levels, k // 32))).repeat(32)
    a = np.empty((k // 512, 16))
    for p in range(k // 512):
        a[p, :8] = np.random.permutation(np.resize(levels, 8))
        for g in range(8):
            far = levels[np.abs(levels - a[p, g]) >= 10]
            a[p, g + 8] = far[np.random.randint(len(far))]
    return np.exp2(a.ravel()).repeat(32)


BF16 = ml_dtypes.bfloat16


def bf(x):
    return np.asarray(x, np.float32).astype(BF16)


def f64(x):
    return np.asarray(x).astype(np.float64)


B, T, C, H = 8, 512, 512, 4
DH = C // H


def rope_tables():
    i = f64(np.arange(1, DH // 2 + 1))
    thetas = np.repeat(1000.0 ** (-2.0 * i / DH), 2)
    pos = f64(np.arange(1, T + 1))
    args = pos[:, None] * thetas[None, :]
    return np.sin(args), np.cos(args)


def apply_rope(u, sin, cos):
    u_odd = u[..., ::2]
    u_even = u[..., 1::2]
    u_sin = np.stack([-u_even, u_odd], axis=-1).reshape(u.shape)
    return u * cos + u_sin * sin


def setup_inputs():
    s = mx_kscale(C)
    return {"x": bf(np.random.standard_normal((B, T, C)) * s),
            "w_qk": bf(np.random.standard_normal((2 * C, C)) / np.sqrt(C) / s[None, :])}


def reference(x, w_qk):
    qk = mxq(f64(x), 2, "e4m3") @ mxq(f64(w_qk), 1, "e4m3").T
    q, k = np.split(qk, 2, axis=-1)
    q = q.reshape(B, T, H, DH).transpose(0, 2, 1, 3)
    k = k.reshape(B, T, H, DH).transpose(0, 2, 1, 3)
    sin, cos = rope_tables()
    return q, k, apply_rope(q, sin, cos), apply_rope(k, sin, cos)

@@ -1,0 +1,258 @@
+import math
+from contextlib import ExitStack
+
+import concourse.mybir as mybir
+from concourse.masks import make_identity
+
+F32 = mybir.dt.float32
+BF16 = mybir.dt.bfloat16
+I32 = mybir.dt.int32
+U32 = mybir.dt.uint32
+U8 = mybir.dt.uint8
+FP8X4 = mybir.dt.float8_e4m3fn_x4
+ALU = mybir.AluOpType
+ACT = mybir.ActivationFunctionType
+
+P = 128
+BATCH, POSITIONS, CHANNELS, HEADS = 8, 512, 512, 4
+HEAD_DIM = CHANNELS // HEADS
+PAIRS = HEAD_DIM // 2
+WORDS = CHANNELS // 2
+HALF_TILES = CHANNELS // P
+SUB = POSITIONS // P
+
+FLOPS = 2 * BATCH * POSITIONS * CHANNELS * 2 * CHANNELS
+
+ROUND_MAGIC = 12582912.0
+
+
+def reduce_rotation_angles(nc, pool):
+    one = pool.tile([P, 1], F32)
+    nc.vector.memset(one[:], 1.0)
+    warm = pool.tile([P, 1], F32)
+    nc.scalar.activation(out=warm[:], in_=one[:], func=ACT.Sin)
+
+    position_int = pool.tile([P, SUB], I32)
+    nc.gpsimd.iota(position_int[:], pattern=[[1, SUB]], base=1, channel_multiplier=SUB)
+    position = pool.tile([P, SUB], F32)
+    nc.vector.tensor_copy(out=position[:], in_=position_int[:])
+
+    ratio = 1000.0 ** (-2.0 / HEAD_DIM)
+    frequency = pool.tile([P, PAIRS], F32)
+    nc.vector.tensor_scalar_mul(out=frequency[:, 0:1], in0=one[:], scalar1=ratio / (2.0 * math.pi))
+    half = 1
+    while half < PAIRS:
+        nc.vector.tensor_scalar_mul(
+            out=frequency[:, half : 2 * half], in0=frequency[:, 0:half], scalar1=ratio**half
+        )
+        half *= 2
+    plus_half_pi = pool.tile([P, 1], F32)
+    nc.vector.tensor_scalar_mul(out=plus_half_pi[:], in0=one[:], scalar1=0.5 * math.pi)
+    minus_half_pi = pool.tile([P, 1], F32)
+    nc.vector.tensor_scalar_mul(out=minus_half_pi[:], in0=one[:], scalar1=-0.5 * math.pi)
+
+    n = SUB * PAIRS
+    turns = pool.tile([P, 2, n], F32)
+    nc.vector.tensor_tensor(
+        out=turns[:, 0, :].rearrange("p (i j) -> p i j", j=PAIRS),
+        in0=position[:].unsqueeze(2).to_broadcast([P, SUB, PAIRS]),
+        in1=frequency[:].unsqueeze(1).to_broadcast([P, SUB, PAIRS]),
+        op=ALU.mult,
+    )
+    nc.vector.tensor_scalar_add(out=turns[:, 1, :], in0=turns[:, 0, :], scalar1=-0.25)
+    whole = pool.tile([P, 2, n], F32)
+    nc.vector.tensor_scalar(
+        out=whole[:],
+        in0=turns[:],
+        scalar1=ROUND_MAGIC,
+        scalar2=ROUND_MAGIC,
+        op0=ALU.add,
+        op1=ALU.subtract,
+    )
+    part = pool.tile([P, 2, n], F32)
+    nc.vector.tensor_tensor(out=part[:], in0=turns[:], in1=whole[:], op=ALU.subtract)
+    size = pool.tile([P, 2, n], F32)
+    nc.vector.scalar_tensor_tensor(
+        out=size[:], in0=part[:], scalar=-1.0, in1=part[:], op0=ALU.mult, op1=ALU.max
+    )
+    return size, plus_half_pi, minus_half_pi
+
+
+def fill_rotation_tables(nc, size, plus_half_pi, minus_half_pi, cos_table, sin_table):
+    n = SUB * PAIRS
+    cos_pairs = cos_table.rearrange("p i (j e) -> p (i j) e", e=2)
+    sin_pairs = sin_table.rearrange("p i (j e) -> p (i j) e", e=2)
+    nc.scalar.activation(
+        out=sin_pairs[:, :, 0:1],
+        in_=size[:, 1, :].unsqueeze(2),
+        func=ACT.Sin,
+        bias=minus_half_pi[:],
+        scale=2.0 * math.pi,
+    )
+    nc.scalar.activation(
+        out=sin_pairs[:, :, 1:2],
+        in_=size[:, 1, :].unsqueeze(2),
+        func=ACT.Sin,
+        bias=plus_half_pi[:],
+        scale=-2.0 * math.pi,
+    )
+    nc.scalar.activation(
+        out=cos_pairs,
+        in_=size[:, 0, :].unsqueeze(2).to_broadcast([P, n, 2]),
+        func=ACT.Sin,
+        bias=plus_half_pi[:],
+        scale=-2.0 * math.pi,
+    )
+
+
+def channels_to_partitions(nc, banks, rows, n_tiles, permutation, grouped):
+    words = rows.bitcast(F32)
+    grouped_words = grouped.bitcast(F32).rearrange("p (t r u) -> p t r u", r=P, u=2)
+    for first in range(0, n_tiles, 2):
+        bank = banks.tile([P, 2, 2, P], F32, tag="transposed")
+        for t in range(2):
+            for u in range(2):
+                start = (first + t) * WORDS
+                nc.tensor.transpose(
+                    bank[:, t, u, :], words[:, start + u : start + WORDS : 2], permutation
+                )
+        nc.scalar.copy(
+            out=grouped_words[:, first : first + 2, :, :],
+            in_=bank[:].rearrange("p t u r -> p t r u"),
+        )
+
+
+def tile_ropeattnlayer_pa_t_kernel(tc, x, w_qk, out_0, out_1, out_2, out_3):
+    nc = tc.nc
+    raw_outs = (out_0, out_1)
+    rotated_outs = (out_2, out_3)
+
+    with ExitStack() as ctx:
+        keep = ctx.enter_context(tc.tile_pool(name="keep", bufs=1))
+        stage = ctx.enter_context(tc.tile_pool(name="stage", bufs=2))
+        terms = ctx.enter_context(tc.tile_pool(name="terms", bufs=3))
+        results = ctx.enter_context(tc.tile_pool(name="results", bufs=4))
+        banks = ctx.enter_context(tc.psum_pool(name="banks", bufs=2))
+        sums = ctx.enter_context(tc.psum_pool(name="sums", bufs=6))
+        ctx.enter_context(tc.manual_schedule())
+
+        x_rows = []
+        for b in range(BATCH):
+            x_rows.append(keep.tile([P, SUB * CHANNELS], BF16, name="x_rows_%d" % b))
+        w_rows = []
+        for s in range(2):
+            w_rows.append(keep.tile([P, HALF_TILES * CHANNELS], BF16, name="w_rows_%d" % s))
+
+        def load_x(b):
+            nc.sync.dma_start(out=x_rows[b][:], in_=x[b].rearrange("(p i) c -> p (i c)", i=SUB))
+
+        def load_w(s):
+            nc.sync.dma_start(
+                out=w_rows[s][:].rearrange("p (t c) -> p t c", c=CHANNELS),
+                in_=w_qk[s * CHANNELS : (s + 1) * CHANNELS, :].rearrange("(t p) c -> p t c", p=P),
+            )
+
+        load_x(0)
+        load_w(0)
+        for b in range(1, BATCH):
+            load_x(b)
+        load_w(1)
+
+        identity = keep.tile([P, P], F32)
+        make_identity(nc, identity[:])
+        swap = keep.tile([P, P], F32)
+        identity_pairs = identity[:].rearrange("p (m s) -> p m s", s=2)
+        swap_pairs = swap[:].rearrange("p (m s) -> p m s", s=2)
+        nc.vector.tensor_copy(out=swap_pairs[:, :, 0:1], in_=identity_pairs[:, :, 1:2])
+        nc.vector.tensor_copy(out=swap_pairs[:, :, 1:2], in_=identity_pairs[:, :, 0:1])
+
+        size, plus_half_pi, minus_half_pi = reduce_rotation_angles(nc, keep)
+
+        x_codes = {}
+        x_scales = {}
+        w_codes = {}
+        w_scales = {}
+
+        def group_x(b):
+            x_grouped = stage.tile([P, POSITIONS * 4], BF16, name="x_grouped", align_bytes=64)
+            x_codes[b] = keep.tile([P, POSITIONS], U32, name="x_codes_%d" % b, align_bytes=64)
+            x_scales[b] = keep.tile([P, POSITIONS], U8, name="x_scales_%d" % b, align_bytes=64)
+            channels_to_partitions(nc, banks, x_rows[b][:], SUB, identity[:], x_grouped[:])
+            return [(x_grouped, x_codes[b], x_scales[b])]
+
+        def group_w(s):
+            grouped = []
+            for kind, permutation in (("partner", swap), ("own", identity)):
+                label = "%s_%d" % (kind, s)
+                w_grouped = stage.tile([P, CHANNELS * 4], BF16, name="w_grouped", align_bytes=64)
+                w_codes[kind, s] = keep.tile([P, CHANNELS], U32, name="w_codes_" + label, align_bytes=64)
+                w_scales[kind, s] = keep.tile([P, CHANNELS], U8, name="w_scales_" + label, align_bytes=64)
+                channels_to_partitions(nc, banks, w_rows[s][:], HALF_TILES, permutation[:], w_grouped[:])
+                grouped.append((w_grouped, w_codes[kind, s], w_scales[kind, s]))
+            return grouped
+
+        def quantise(grouped):
+            for values, codes, scales in grouped:
+                nc.vector.quantize_mx(out=codes[:].bitcast(FP8X4), scales=scales[:], in_=values[:])
+
+        quantise(group_x(0) + group_w(0))
+
+        cos_table = keep.tile([P, SUB, HEAD_DIM], F32)
+        sin_table = keep.tile([P, SUB, HEAD_DIM], F32)
+        fill_rotation_tables(nc, size, plus_half_pi, minus_half_pi, cos_table[:], sin_table[:])
+
+        for s in range(2):
+            for b in range(BATCH):
+                grouped = []
+                if s == 0:
+                    grouped = group_x(b + 1) if b + 1 < BATCH else group_w(1)
+                raw = results.tile([P, HEADS, SUB, HEAD_DIM], F32, name="raw")
+                rotated = results.tile([P, HEADS, SUB, HEAD_DIM], F32, name="rotated")
+                for first in range(0, SUB, 2):
+                    product = {}
+                    for kind in ("partner", "own"):
+                        for i in (first, first + 1):
+                            tokens = slice(i * P, (i + 1) * P)
+                            product[kind, i] = sums.tile([P, HEADS, HEAD_DIM], F32, name="product")
+                            nc.tensor.matmul_mx(
+                                out=product[kind, i][:].rearrange("p h f -> p (h f)"),
+                                lhsT=x_codes[b][:, tokens].bitcast(FP8X4),
+                                lhsT_scale=x_scales[b][:, tokens],
+                                rhs=w_codes[kind, s][:].bitcast(FP8X4),
+                                rhs_scale=w_scales[kind, s][:],
+                                start=True,
+                                stop=True,
+                            )
+                    straight = terms.tile([P, 2, HEADS, HEAD_DIM], F32, name="straight")
+                    crossed = terms.tile([P, 2, HEADS, HEAD_DIM], F32, name="crossed")
+                    for i in (first, first + 1):
+                        nc.scalar.copy(out=raw[:, :, i, :], in_=product["own", i][:])
+                        nc.vector.tensor_tensor(
+                            out=crossed[:, i - first, :, :],
+                            in0=product["partner", i][:],
+                            in1=sin_table[:, i : i + 1, :].to_broadcast([P, HEADS, HEAD_DIM]),
+                            op=ALU.mult,
+                        )
+                    for i in (first, first + 1):
+                        nc.vector.tensor_tensor(
+                            out=straight[:, i - first, :, :],
+                            in0=product["own", i][:],
+                            in1=cos_table[:, i : i + 1, :].to_broadcast([P, HEADS, HEAD_DIM]),
+                            op=ALU.mult,
+                        )
+                    nc.gpsimd.tensor_tensor(
+                        out=rotated[:, :, first : first + 2, :],
+                        in0=straight[:].rearrange("p i h f -> p h i f"),
+                        in1=crossed[:].rearrange("p i h f -> p h i f"),
+                        op=ALU.add,
+                    )
+                    if first == 0:
+                        quantise(grouped)
+                nc.sync.dma_start(
+                    out=raw_outs[s][b].rearrange("h (p i) f -> p h (i f)", i=SUB),
+                    in_=raw[:].rearrange("p h i f -> p h (i f)"),
+                )
+                nc.sync.dma_start(
+                    out=rotated_outs[s][b].rearrange("h (p i) f -> p h (i f)", i=SUB),
+                    in_=rotated[:].rearrange("p h i f -> p h (i f)"),
+                )

@@ -17,8 +17,8 @@ P = 128
 BATCH, POSITIONS, CHANNELS, HEADS = 8, 512, 512, 4
 HEAD_DIM = CHANNELS // HEADS
 PAIRS = HEAD_DIM // 2
+ALL_PAIRS = HEADS * PAIRS
 WORDS = CHANNELS // 2
-HALF_TILES = CHANNELS // P
 SUB = POSITIONS // P
 
 FLOPS = 2 * BATCH * POSITIONS * CHANNELS * 2 * CHANNELS
@@ -26,16 +26,14 @@ FLOPS = 2 * BATCH * POSITIONS * CHANNELS * 2 * CHANNELS
 ROUND_MAGIC = 12582912.0
 
 
-def reduce_rotation_angles(nc, pool):
+def rotation_tables(nc, pool):
+    position_int = pool.tile([P, SUB], I32)
+    nc.gpsimd.iota(position_int[:], pattern=[[1, SUB]], base=1, channel_multiplier=SUB)
+
     one = pool.tile([P, 1], F32)
     nc.vector.memset(one[:], 1.0)
     warm = pool.tile([P, 1], F32)
     nc.scalar.activation(out=warm[:], in_=one[:], func=ACT.Sin)
-
-    position_int = pool.tile([P, SUB], I32)
-    nc.gpsimd.iota(position_int[:], pattern=[[1, SUB]], base=1, channel_multiplier=SUB)
-    position = pool.tile([P, SUB], F32)
-    nc.vector.tensor_copy(out=position[:], in_=position_int[:])
 
     ratio = 1000.0 ** (-2.0 / HEAD_DIM)
     frequency = pool.tile([P, PAIRS], F32)
@@ -50,17 +48,17 @@ def reduce_rotation_angles(nc, pool):
     nc.vector.tensor_scalar_mul(out=plus_half_pi[:], in0=one[:], scalar1=0.5 * math.pi)
     minus_half_pi = pool.tile([P, 1], F32)
     nc.vector.tensor_scalar_mul(out=minus_half_pi[:], in0=one[:], scalar1=-0.5 * math.pi)
+    position = pool.tile([P, SUB], F32)
+    nc.vector.tensor_copy(out=position[:], in_=position_int[:])
 
-    n = SUB * PAIRS
-    turns = pool.tile([P, 2, n], F32)
+    turns = pool.tile([P, SUB, PAIRS], F32)
     nc.vector.tensor_tensor(
-        out=turns[:, 0, :].rearrange("p (i j) -> p i j", j=PAIRS),
+        out=turns[:],
         in0=position[:].unsqueeze(2).to_broadcast([P, SUB, PAIRS]),
         in1=frequency[:].unsqueeze(1).to_broadcast([P, SUB, PAIRS]),
         op=ALU.mult,
     )
-    nc.vector.tensor_scalar_add(out=turns[:, 1, :], in0=turns[:, 0, :], scalar1=-0.25)
-    whole = pool.tile([P, 2, n], F32)
+    whole = pool.tile([P, SUB, PAIRS], F32)
     nc.vector.tensor_scalar(
         out=whole[:],
         in0=turns[:],
@@ -69,57 +67,29 @@ def reduce_rotation_angles(nc, pool):
         op0=ALU.add,
         op1=ALU.subtract,
     )
-    part = pool.tile([P, 2, n], F32)
+    part = pool.tile([P, SUB, PAIRS], F32)
     nc.vector.tensor_tensor(out=part[:], in0=turns[:], in1=whole[:], op=ALU.subtract)
-    size = pool.tile([P, 2, n], F32)
+    size = pool.tile([P, SUB, PAIRS], F32)
     nc.vector.scalar_tensor_tensor(
         out=size[:], in0=part[:], scalar=-1.0, in1=part[:], op0=ALU.mult, op1=ALU.max
     )
-    return size, plus_half_pi, minus_half_pi
 
-
-def fill_rotation_tables(nc, size, plus_half_pi, minus_half_pi, cos_table, sin_table):
-    n = SUB * PAIRS
-    cos_pairs = cos_table.rearrange("p i (j e) -> p (i j) e", e=2)
-    sin_pairs = sin_table.rearrange("p i (j e) -> p (i j) e", e=2)
+    sine = pool.tile([P, SUB, PAIRS], F32)
+    nc.scalar.activation(out=sine[:], in_=part[:], func=ACT.Sin, scale=2.0 * math.pi)
+    minus_cosine = pool.tile([P, SUB, PAIRS], F32)
     nc.scalar.activation(
-        out=sin_pairs[:, :, 0:1],
-        in_=size[:, 1, :].unsqueeze(2),
-        func=ACT.Sin,
-        bias=minus_half_pi[:],
-        scale=2.0 * math.pi,
+        out=minus_cosine[:], in_=size[:], func=ACT.Sin, bias=minus_half_pi[:], scale=2.0 * math.pi
     )
+    cosine = pool.tile([P, SUB, PAIRS], F32)
     nc.scalar.activation(
-        out=sin_pairs[:, :, 1:2],
-        in_=size[:, 1, :].unsqueeze(2),
-        func=ACT.Sin,
-        bias=plus_half_pi[:],
-        scale=-2.0 * math.pi,
+        out=cosine[:], in_=size[:], func=ACT.Sin, bias=plus_half_pi[:], scale=-2.0 * math.pi
     )
-    nc.scalar.activation(
-        out=cos_pairs,
-        in_=size[:, 0, :].unsqueeze(2).to_broadcast([P, n, 2]),
-        func=ACT.Sin,
-        bias=plus_half_pi[:],
-        scale=-2.0 * math.pi,
+    cross = pool.tile([P, SUB, PAIRS, 2], F32)
+    nc.gpsimd.tensor_tensor(
+        out=cross[:, :, :, 0], in0=minus_cosine[:], in1=sine[:], op=ALU.subtract
     )
-
-
-def channels_to_partitions(nc, banks, rows, n_tiles, permutation, grouped):
-    words = rows.bitcast(F32)
-    grouped_words = grouped.bitcast(F32).rearrange("p (t r u) -> p t r u", r=P, u=2)
-    for first in range(0, n_tiles, 2):
-        bank = banks.tile([P, 2, 2, P], F32, tag="transposed")
-        for t in range(2):
-            for u in range(2):
-                start = (first + t) * WORDS
-                nc.tensor.transpose(
-                    bank[:, t, u, :], words[:, start + u : start + WORDS : 2], permutation
-                )
-        nc.scalar.copy(
-            out=grouped_words[:, first : first + 2, :, :],
-            in_=bank[:].rearrange("p t u r -> p t r u"),
-        )
+    nc.gpsimd.tensor_tensor(out=cross[:, :, :, 1], in0=minus_cosine[:], in1=sine[:], op=ALU.add)
+    return cosine, cross
 
 
 def tile_ropeattnlayer_pa_t_kernel(tc, x, w_qk, out_0, out_1, out_2, out_3):
@@ -131,126 +101,189 @@ def tile_ropeattnlayer_pa_t_kernel(tc, x, w_qk, out_0, out_1, out_2, out_3):
         keep = ctx.enter_context(tc.tile_pool(name="keep", bufs=1))
         stage = ctx.enter_context(tc.tile_pool(name="stage", bufs=2))
         terms = ctx.enter_context(tc.tile_pool(name="terms", bufs=3))
-        results = ctx.enter_context(tc.tile_pool(name="results", bufs=4))
+        results = ctx.enter_context(tc.tile_pool(name="results", bufs=5))
         banks = ctx.enter_context(tc.psum_pool(name="banks", bufs=2))
-        sums = ctx.enter_context(tc.psum_pool(name="sums", bufs=6))
+        products = ctx.enter_context(tc.psum_pool(name="products", bufs=4))
+        sums = ctx.enter_context(tc.psum_pool(name="sums", bufs=2))
         ctx.enter_context(tc.manual_schedule())
 
         x_rows = []
         for b in range(BATCH):
-            x_rows.append(keep.tile([P, SUB * CHANNELS], BF16, name="x_rows_%d" % b))
+            x_rows.append(keep.tile([P, SUB, CHANNELS], BF16, name="x_rows_%d" % b))
         w_rows = []
         for s in range(2):
-            w_rows.append(keep.tile([P, HALF_TILES * CHANNELS], BF16, name="w_rows_%d" % s))
+            w_rows.append(keep.tile([P, 2, 2, CHANNELS], BF16, name="w_rows_%d" % s))
 
-        def load_x(b):
-            nc.sync.dma_start(out=x_rows[b][:], in_=x[b].rearrange("(p i) c -> p (i c)", i=SUB))
-
-        def load_w(s):
+        def load_x(b, first, last):
             nc.sync.dma_start(
-                out=w_rows[s][:].rearrange("p (t c) -> p t c", c=CHANNELS),
-                in_=w_qk[s * CHANNELS : (s + 1) * CHANNELS, :].rearrange("(t p) c -> p t c", p=P),
+                out=x_rows[b][:, first:last, :],
+                in_=x[b].rearrange("(p i) c -> p i c", i=SUB)[:, first:last, :],
             )
 
-        load_x(0)
-        load_w(0)
+        def load_w(s, g):
+            start = s * CHANNELS + g * 2 * P
+            nc.sync.dma_start(
+                out=w_rows[s][:, g, :, :],
+                in_=w_qk[start : start + 2 * P, :].rearrange("(p a) c -> p a c", a=2),
+            )
+
+        load_w(0, 0)
+        load_w(0, 1)
+        load_x(0, 0, 2)
+        load_x(0, 2, 4)
         for b in range(1, BATCH):
-            load_x(b)
-        load_w(1)
+            load_x(b, 0, SUB)
+        load_w(1, 0)
+        load_w(1, 1)
 
         identity = keep.tile([P, P], F32)
         make_identity(nc, identity[:])
-        swap = keep.tile([P, P], F32)
-        identity_pairs = identity[:].rearrange("p (m s) -> p m s", s=2)
-        swap_pairs = swap[:].rearrange("p (m s) -> p m s", s=2)
-        nc.vector.tensor_copy(out=swap_pairs[:, :, 0:1], in_=identity_pairs[:, :, 1:2])
-        nc.vector.tensor_copy(out=swap_pairs[:, :, 1:2], in_=identity_pairs[:, :, 0:1])
 
-        size, plus_half_pi, minus_half_pi = reduce_rotation_angles(nc, keep)
+        def turn(tiles):
+            bank = banks.tile([P, 2, 2, P], F32, name="bank")
+            for t in range(2):
+                words = tiles[t].bitcast(F32)
+                for u in range(2):
+                    nc.tensor.transpose(bank[:, t, u, :], words[:, u:WORDS:2], identity[:])
+            return bank
 
-        x_codes = {}
-        x_scales = {}
-        w_codes = {}
-        w_scales = {}
+        def spread(copy, bank, grouped):
+            copy(
+                out=grouped.bitcast(F32).rearrange("p t (r u) -> p t r u", u=2),
+                in_=bank[:].rearrange("p t u r -> p t r u"),
+            )
 
-        def group_x(b):
-            x_grouped = stage.tile([P, POSITIONS * 4], BF16, name="x_grouped", align_bytes=64)
-            x_codes[b] = keep.tile([P, POSITIONS], U32, name="x_codes_%d" % b, align_bytes=64)
-            x_scales[b] = keep.tile([P, POSITIONS], U8, name="x_scales_%d" % b, align_bytes=64)
-            channels_to_partitions(nc, banks, x_rows[b][:], SUB, identity[:], x_grouped[:])
-            return [(x_grouped, x_codes[b], x_scales[b])]
+        def quantise(grouped, codes, scales, columns):
+            nc.vector.quantize_mx(
+                out=codes[:, columns].bitcast(FP8X4), scales=scales[:, columns], in_=grouped
+            )
 
-        def group_w(s):
-            grouped = []
-            for kind, permutation in (("partner", swap), ("own", identity)):
-                label = "%s_%d" % (kind, s)
-                w_grouped = stage.tile([P, CHANNELS * 4], BF16, name="w_grouped", align_bytes=64)
-                w_codes[kind, s] = keep.tile([P, CHANNELS], U32, name="w_codes_" + label, align_bytes=64)
-                w_scales[kind, s] = keep.tile([P, CHANNELS], U8, name="w_scales_" + label, align_bytes=64)
-                channels_to_partitions(nc, banks, w_rows[s][:], HALF_TILES, permutation[:], w_grouped[:])
-                grouped.append((w_grouped, w_codes[kind, s], w_scales[kind, s]))
-            return grouped
+        x_codes = []
+        x_scales = []
+        for b in range(BATCH):
+            x_codes.append(keep.tile([P, POSITIONS], U32, name="x_codes_%d" % b, align_bytes=64))
+            x_scales.append(keep.tile([P, POSITIONS], U8, name="x_scales_%d" % b, align_bytes=64))
+        w_codes = []
+        w_scales = []
+        for s in range(2):
+            w_codes.append(keep.tile([P, CHANNELS], U32, name="w_codes_%d" % s, align_bytes=64))
+            w_scales.append(keep.tile([P, CHANNELS], U8, name="w_scales_%d" % s, align_bytes=64))
 
-        def quantise(grouped):
-            for values, codes, scales in grouped:
-                nc.vector.quantize_mx(out=codes[:].bitcast(FP8X4), scales=scales[:], in_=values[:])
+        def turn_x(b, pair):
+            return turn([x_rows[b][:, 2 * pair + t, :] for t in range(2)])
 
-        quantise(group_x(0) + group_w(0))
+        def turn_w(s, g):
+            return turn([w_rows[s][:, g, a, :] for a in range(2)])
 
-        cos_table = keep.tile([P, SUB, HEAD_DIM], F32)
-        sin_table = keep.tile([P, SUB, HEAD_DIM], F32)
-        fill_rotation_tables(nc, size, plus_half_pi, minus_half_pi, cos_table[:], sin_table[:])
+        def x_stage():
+            return stage.tile([P, SUB, 4 * P], BF16, name="x_grouped", align_bytes=64)
+
+        def w_stage():
+            return stage.tile([P, 2, 2, 4 * P], BF16, name="w_grouped", align_bytes=64)
+
+        w_grouped = w_stage()
+        x_grouped = x_stage()
+        cosine, cross = rotation_tables(nc, keep)
+        bank = turn_w(0, 0)
+        spread(nc.scalar.copy, bank, w_grouped[:, :, 0, :])
+        bank = turn_w(0, 1)
+        spread(nc.vector.tensor_copy, bank, w_grouped[:, :, 1, :])
+        bank = turn_x(0, 0)
+        spread(nc.scalar.copy, bank, x_grouped[:, 0:2, :])
+        quantise(
+            w_grouped[:].rearrange("p a g v -> p (a g v)"), w_codes[0], w_scales[0], slice(0, CHANNELS)
+        )
+        bank = turn_x(0, 1)
+        spread(nc.scalar.copy, bank, x_grouped[:, 2:4, :])
+        for pair in range(2):
+            quantise(
+                x_grouped[:, 2 * pair : 2 * pair + 2, :].rearrange("p i v -> p (i v)"),
+                x_codes[0],
+                x_scales[0],
+                slice(pair * 2 * P, (pair + 1) * 2 * P),
+            )
+
+        def group_next(b):
+            if b + 1 < BATCH:
+                x_grouped = x_stage()
+                for pair in range(2):
+                    spread(nc.scalar.copy, turn_x(b + 1, pair), x_grouped[:, 2 * pair : 2 * pair + 2, :])
+                values = x_grouped[:].rearrange("p i v -> p (i v)")
+                return (values, x_codes[b + 1], x_scales[b + 1], slice(0, POSITIONS))
+            w_grouped = w_stage()
+            for g in range(2):
+                spread(nc.scalar.copy, turn_w(1, g), w_grouped[:, :, g, :])
+            values = w_grouped[:].rearrange("p a g v -> p (a g v)")
+            return (values, w_codes[1], w_scales[1], slice(0, CHANNELS))
 
         for s in range(2):
             for b in range(BATCH):
-                grouped = []
+                grouped = None
                 if s == 0:
-                    grouped = group_x(b + 1) if b + 1 < BATCH else group_w(1)
-                raw = results.tile([P, HEADS, SUB, HEAD_DIM], F32, name="raw")
+                    grouped = group_next(b)
+                raw = results.tile([P, HEADS, SUB, PAIRS, 2], F32, name="raw")
                 rotated = results.tile([P, HEADS, SUB, HEAD_DIM], F32, name="rotated")
                 for first in range(0, SUB, 2):
-                    product = {}
-                    for kind in ("partner", "own"):
-                        for i in (first, first + 1):
-                            tokens = slice(i * P, (i + 1) * P)
-                            product[kind, i] = sums.tile([P, HEADS, HEAD_DIM], F32, name="product")
+                    pair_sum = sums.tile([P, 2, ALL_PAIRS], F32, name="pair_sum")
+                    product = []
+                    for i in (first, first + 1):
+                        tokens = slice(i * P, (i + 1) * P)
+                        own = products.tile([P, 2, ALL_PAIRS], F32, name="own")
+                        product.append(own)
+                        passes = [(own[:].rearrange("p a m -> p (a m)"), slice(0, CHANNELS), True, True)]
+                        for a in range(2):
+                            columns = slice(a * ALL_PAIRS, (a + 1) * ALL_PAIRS)
+                            passes.append((pair_sum[:, i - first, :], columns, a == 0, a == 1))
+                        for out, columns, start, stop in passes:
                             nc.tensor.matmul_mx(
-                                out=product[kind, i][:].rearrange("p h f -> p (h f)"),
+                                out=out,
                                 lhsT=x_codes[b][:, tokens].bitcast(FP8X4),
                                 lhsT_scale=x_scales[b][:, tokens],
-                                rhs=w_codes[kind, s][:].bitcast(FP8X4),
-                                rhs_scale=w_scales[kind, s][:],
-                                start=True,
-                                stop=True,
+                                rhs=w_codes[s][:, columns].bitcast(FP8X4),
+                                rhs_scale=w_scales[s][:, columns],
+                                start=start,
+                                stop=stop,
                             )
-                    straight = terms.tile([P, 2, HEADS, HEAD_DIM], F32, name="straight")
-                    crossed = terms.tile([P, 2, HEADS, HEAD_DIM], F32, name="crossed")
-                    for i in (first, first + 1):
-                        nc.scalar.copy(out=raw[:, :, i, :], in_=product["own", i][:])
+
+                    def copy_raw(i):
+                        nc.scalar.copy(
+                            out=raw[:, :, i, :, :],
+                            in_=product[i - first][:].rearrange("p a (h m) -> p h m a", h=HEADS),
+                        )
+
+                    straight = terms.tile([P, 2, HEADS, PAIRS], F32, name="straight")
+                    crossed = terms.tile([P, 2, HEADS, PAIRS, 2], F32, name="crossed")
+
+                    def multiply_crossed(i):
                         nc.vector.tensor_tensor(
-                            out=crossed[:, i - first, :, :],
-                            in0=product["partner", i][:],
-                            in1=sin_table[:, i : i + 1, :].to_broadcast([P, HEADS, HEAD_DIM]),
+                            out=crossed[:, i - first, :, :, :],
+                            in0=product[i - first][:, ::-1, :].rearrange("p a (h m) -> p h m a", h=HEADS),
+                            in1=cross[:, i, :, :].unsqueeze(1).to_broadcast([P, HEADS, PAIRS, 2]),
                             op=ALU.mult,
                         )
-                    for i in (first, first + 1):
-                        nc.vector.tensor_tensor(
-                            out=straight[:, i - first, :, :],
-                            in0=product["own", i][:],
-                            in1=cos_table[:, i : i + 1, :].to_broadcast([P, HEADS, HEAD_DIM]),
-                            op=ALU.mult,
-                        )
-                    nc.gpsimd.tensor_tensor(
-                        out=rotated[:, :, first : first + 2, :],
-                        in0=straight[:].rearrange("p i h f -> p h i f"),
-                        in1=crossed[:].rearrange("p i h f -> p h i f"),
-                        op=ALU.add,
+
+                    copy_raw(first)
+                    nc.vector.tensor_tensor(
+                        out=straight[:],
+                        in0=pair_sum[:].rearrange("p i (h m) -> p i h m", h=HEADS),
+                        in1=cosine[:, first : first + 2, :].unsqueeze(2).to_broadcast([P, 2, HEADS, PAIRS]),
+                        op=ALU.mult,
                     )
-                    if first == 0:
-                        quantise(grouped)
+                    multiply_crossed(first)
+                    copy_raw(first + 1)
+                    multiply_crossed(first + 1)
+                    for i in (first, first + 1):
+                        nc.gpsimd.tensor_tensor(
+                            out=rotated[:, :, i, :].rearrange("p h (m a) -> p h m a", a=2),
+                            in0=straight[:, i - first, :, :].unsqueeze(3).to_broadcast([P, HEADS, PAIRS, 2]),
+                            in1=crossed[:, i - first, :, :, :],
+                            op=ALU.add,
+                        )
+                    if first == 0 and grouped is not None:
+                        quantise(*grouped)
                 nc.sync.dma_start(
                     out=raw_outs[s][b].rearrange("h (p i) f -> p h (i f)", i=SUB),
-                    in_=raw[:].rearrange("p h i f -> p h (i f)"),
+                    in_=raw[:].rearrange("p h i m a -> p h (i m a)"),
                 )
                 nc.sync.dma_start(
                     out=rotated_outs[s][b].rearrange("h (p i) f -> p h (i f)", i=SUB),

@@ -23,6 +23,8 @@ SUB = POSITIONS // P
 
 FLOPS = 2 * BATCH * POSITIONS * CHANNELS * 2 * CHANNELS
 
+VECTOR_ADDS = 2
+
 ROUND_MAGIC = 12582912.0
 
 
@@ -273,7 +275,8 @@ def tile_ropeattnlayer_pa_t_kernel(tc, x, w_qk, out_0, out_1, out_2, out_3):
                     copy_raw(first + 1)
                     multiply_crossed(first + 1)
                     for i in (first, first + 1):
-                        nc.gpsimd.tensor_tensor(
+                        adder = nc.vector if i == VECTOR_ADDS else nc.gpsimd
+                        adder.tensor_tensor(
                             out=rotated[:, :, i, :].rearrange("p h (m a) -> p h m a", a=2),
                             in0=straight[:, i - first, :, :].unsqueeze(3).to_broadcast([P, HEADS, PAIRS, 2]),
                             in1=crossed[:, i - first, :, :, :],

@@ -23,8 +23,6 @@ SUB = POSITIONS // P
 
 FLOPS = 2 * BATCH * POSITIONS * CHANNELS * 2 * CHANNELS
 
-VECTOR_ADDS = 2
-
 ROUND_MAGIC = 12582912.0
 
 
@@ -275,7 +273,7 @@ def tile_ropeattnlayer_pa_t_kernel(tc, x, w_qk, out_0, out_1, out_2, out_3):
                     copy_raw(first + 1)
                     multiply_crossed(first + 1)
                     for i in (first, first + 1):
-                        adder = nc.vector if i == VECTOR_ADDS else nc.gpsimd
+                        adder = nc.vector if i == first else nc.gpsimd
                         adder.tensor_tensor(
                             out=rotated[:, :, i, :].rearrange("p h (m a) -> p h m a", a=2),
                             in0=straight[:, i - first, :, :].unsqueeze(3).to_broadcast([P, HEADS, PAIRS, 2]),

@@ -26,7 +26,7 @@ FLOPS = 2 * BATCH * POSITIONS * CHANNELS * 2 * CHANNELS
 ROUND_MAGIC = 12582912.0
 
 
-def rotation_tables(nc, pool):
+def reduce_angles(nc, pool):
     position_int = pool.tile([P, SUB], I32)
     nc.gpsimd.iota(position_int[:], pattern=[[1, SUB]], base=1, channel_multiplier=SUB)
 
@@ -74,6 +74,10 @@ def rotation_tables(nc, pool):
         out=size[:], in0=part[:], scalar=-1.0, in1=part[:], op0=ALU.mult, op1=ALU.max
     )
 
+    return part, size, plus_half_pi, minus_half_pi
+
+
+def rotation_tables(nc, pool, part, size, plus_half_pi, minus_half_pi):
     sine = pool.tile([P, SUB, PAIRS], F32)
     nc.scalar.activation(out=sine[:], in_=part[:], func=ACT.Sin, scale=2.0 * math.pi)
     minus_cosine = pool.tile([P, SUB, PAIRS], F32)
@@ -100,7 +104,7 @@ def tile_ropeattnlayer_pa_t_kernel(tc, x, w_qk, out_0, out_1, out_2, out_3):
     with ExitStack() as ctx:
         keep = ctx.enter_context(tc.tile_pool(name="keep", bufs=1))
         stage = ctx.enter_context(tc.tile_pool(name="stage", bufs=2))
-        terms = ctx.enter_context(tc.tile_pool(name="terms", bufs=3))
+        terms = ctx.enter_context(tc.tile_pool(name="terms", bufs=2))
         results = ctx.enter_context(tc.tile_pool(name="results", bufs=5))
         banks = ctx.enter_context(tc.psum_pool(name="banks", bufs=2))
         products = ctx.enter_context(tc.psum_pool(name="products", bufs=4))
@@ -139,13 +143,11 @@ def tile_ropeattnlayer_pa_t_kernel(tc, x, w_qk, out_0, out_1, out_2, out_3):
         identity = keep.tile([P, P], F32)
         make_identity(nc, identity[:])
 
-        def turn(tiles):
-            bank = banks.tile([P, 2, 2, P], F32, name="bank")
+        def turn(tiles, bank):
             for t in range(2):
                 words = tiles[t].bitcast(F32)
                 for u in range(2):
                     nc.tensor.transpose(bank[:, t, u, :], words[:, u:WORDS:2], identity[:])
-            return bank
 
         def spread(copy, bank, grouped):
             copy(
@@ -169,11 +171,11 @@ def tile_ropeattnlayer_pa_t_kernel(tc, x, w_qk, out_0, out_1, out_2, out_3):
             w_codes.append(keep.tile([P, CHANNELS], U32, name="w_codes_%d" % s, align_bytes=64))
             w_scales.append(keep.tile([P, CHANNELS], U8, name="w_scales_%d" % s, align_bytes=64))
 
-        def turn_x(b, pair):
-            return turn([x_rows[b][:, 2 * pair + t, :] for t in range(2)])
+        def x_tiles(b, pair):
+            return [x_rows[b][:, 2 * pair + t, :] for t in range(2)]
 
-        def turn_w(s, g):
-            return turn([w_rows[s][:, g, a, :] for a in range(2)])
+        def w_tiles(s, g):
+            return [w_rows[s][:, g, a, :] for a in range(2)]
 
         def x_stage():
             return stage.tile([P, SUB, 4 * P], BF16, name="x_grouped", align_bytes=64)
@@ -183,18 +185,25 @@ def tile_ropeattnlayer_pa_t_kernel(tc, x, w_qk, out_0, out_1, out_2, out_3):
 
         w_grouped = w_stage()
         x_grouped = x_stage()
-        cosine, cross = rotation_tables(nc, keep)
-        bank = turn_w(0, 0)
-        spread(nc.scalar.copy, bank, w_grouped[:, :, 0, :])
-        bank = turn_w(0, 1)
-        spread(nc.vector.tensor_copy, bank, w_grouped[:, :, 1, :])
-        bank = turn_x(0, 0)
-        spread(nc.scalar.copy, bank, x_grouped[:, 0:2, :])
+        part, size, plus_half_pi, minus_half_pi = reduce_angles(nc, keep)
+        w_banks = []
+        x_banks = []
+        for g in range(2):
+            w_bank = banks.tile([P, 2, 2, P], F32, name="bank")
+            turn(w_tiles(0, g), w_bank)
+            w_banks.append(w_bank)
+        for pair in range(2):
+            x_bank = products.tile([P, 2, 2, P], F32, name="own")
+            turn(x_tiles(0, pair), x_bank)
+            x_banks.append(x_bank)
+        spread(nc.scalar.copy, w_banks[0], w_grouped[:, :, 0, :])
+        spread(nc.vector.tensor_copy, w_banks[1], w_grouped[:, :, 1, :])
+        cosine, cross = rotation_tables(nc, keep, part, size, plus_half_pi, minus_half_pi)
+        for pair in range(2):
+            spread(nc.scalar.copy, x_banks[pair], x_grouped[:, 2 * pair : 2 * pair + 2, :])
         quantise(
             w_grouped[:].rearrange("p a g v -> p (a g v)"), w_codes[0], w_scales[0], slice(0, CHANNELS)
         )
-        bank = turn_x(0, 1)
-        spread(nc.scalar.copy, bank, x_grouped[:, 2:4, :])
         for pair in range(2):
             quantise(
                 x_grouped[:, 2 * pair : 2 * pair + 2, :].rearrange("p i v -> p (i v)"),
@@ -203,90 +212,124 @@ def tile_ropeattnlayer_pa_t_kernel(tc, x, w_qk, out_0, out_1, out_2, out_3):
                 slice(pair * 2 * P, (pair + 1) * 2 * P),
             )
 
-        def group_next(b):
+        def next_operand(b):
             if b + 1 < BATCH:
                 x_grouped = x_stage()
-                for pair in range(2):
-                    spread(nc.scalar.copy, turn_x(b + 1, pair), x_grouped[:, 2 * pair : 2 * pair + 2, :])
+                tiles = [x_tiles(b + 1, pair) for pair in range(2)]
+                places = [x_grouped[:, 2 * pair : 2 * pair + 2, :] for pair in range(2)]
                 values = x_grouped[:].rearrange("p i v -> p (i v)")
-                return (values, x_codes[b + 1], x_scales[b + 1], slice(0, POSITIONS))
+                return tiles, places, (values, x_codes[b + 1], x_scales[b + 1], slice(0, POSITIONS))
             w_grouped = w_stage()
-            for g in range(2):
-                spread(nc.scalar.copy, turn_w(1, g), w_grouped[:, :, g, :])
+            tiles = [w_tiles(1, g) for g in range(2)]
+            places = [w_grouped[:, :, g, :] for g in range(2)]
             values = w_grouped[:].rearrange("p a g v -> p (a g v)")
-            return (values, w_codes[1], w_scales[1], slice(0, CHANNELS))
+            return tiles, places, (values, w_codes[1], w_scales[1], slice(0, CHANNELS))
 
+        def multiply(s, b, i, columns, out, start, stop):
+            tokens = slice(i * P, (i + 1) * P)
+            nc.tensor.matmul_mx(
+                out=out,
+                lhsT=x_codes[b][:, tokens].bitcast(FP8X4),
+                lhsT_scale=x_scales[b][:, tokens],
+                rhs=w_codes[s][:, columns].bitcast(FP8X4),
+                rhs_scale=w_scales[s][:, columns],
+                start=start,
+                stop=stop,
+            )
+
+        def sum_pairs(s, b, first):
+            pair_sum = sums.tile([P, 2, ALL_PAIRS], F32, name="pair_sum")
+            for t in range(2):
+                for a in range(2):
+                    columns = slice(a * ALL_PAIRS, (a + 1) * ALL_PAIRS)
+                    multiply(s, b, first + t, columns, pair_sum[:, t, :], a == 0, a == 1)
+            return pair_sum
+
+        def project(s, b, i):
+            own = products.tile([P, 2, ALL_PAIRS], F32, name="own")
+            multiply(s, b, i, slice(0, CHANNELS), own[:].rearrange("p a m -> p (a m)"), True, True)
+            return own
+
+        def copy_raw(own, raw_pairs, i):
+            nc.scalar.copy(
+                out=raw_pairs[:, :, i, :, :],
+                in_=own[:].rearrange("p a (h m) -> p h m a", h=HEADS),
+            )
+
+        def multiply_straight(pair_sum, first, straight):
+            nc.vector.tensor_tensor(
+                out=straight[:],
+                in0=pair_sum[:].rearrange("p i (h m) -> p i h m", h=HEADS),
+                in1=cosine[:, first : first + 2, :].unsqueeze(2).to_broadcast([P, 2, HEADS, PAIRS]),
+                op=ALU.mult,
+            )
+
+        def multiply_crossed(own, i, crossed):
+            nc.vector.tensor_tensor(
+                out=crossed,
+                in0=own[:, ::-1, :].rearrange("p a (h m) -> p h m a", h=HEADS),
+                in1=cross[:, i, :, :].unsqueeze(1).to_broadcast([P, HEADS, PAIRS, 2]),
+                op=ALU.mult,
+            )
+
+        def add(engine, straight, crossed, rotated, first):
+            for t in range(2):
+                engine.tensor_tensor(
+                    out=rotated[:, :, first + t, :].rearrange("p h (m a) -> p h m a", a=2),
+                    in0=straight[:, t, :, :].unsqueeze(3).to_broadcast([P, HEADS, PAIRS, 2]),
+                    in1=crossed[:, t, :, :, :],
+                    op=ALU.add,
+                )
+
+        def store(outs, b, result):
+            nc.sync.dma_start(
+                out=outs[b].rearrange("h (p i) f -> p h (i f)", i=SUB),
+                in_=result[:].rearrange("p h i f -> p h (i f)"),
+            )
+
+        late = None
         for s in range(2):
             for b in range(BATCH):
-                grouped = None
-                if s == 0:
-                    grouped = group_next(b)
-                raw = results.tile([P, HEADS, SUB, PAIRS, 2], F32, name="raw")
+                raw = results.tile([P, HEADS, SUB, HEAD_DIM], F32, name="raw")
+                raw_pairs = raw[:].rearrange("p h i (m a) -> p h i m a", a=2)
                 rotated = results.tile([P, HEADS, SUB, HEAD_DIM], F32, name="rotated")
-                for first in range(0, SUB, 2):
-                    pair_sum = sums.tile([P, 2, ALL_PAIRS], F32, name="pair_sum")
-                    product = []
-                    for i in (first, first + 1):
-                        tokens = slice(i * P, (i + 1) * P)
-                        own = products.tile([P, 2, ALL_PAIRS], F32, name="own")
-                        product.append(own)
-                        passes = [(own[:].rearrange("p a m -> p (a m)"), slice(0, CHANNELS), True, True)]
-                        for a in range(2):
-                            columns = slice(a * ALL_PAIRS, (a + 1) * ALL_PAIRS)
-                            passes.append((pair_sum[:, i - first, :], columns, a == 0, a == 1))
-                        for out, columns, start, stop in passes:
-                            nc.tensor.matmul_mx(
-                                out=out,
-                                lhsT=x_codes[b][:, tokens].bitcast(FP8X4),
-                                lhsT_scale=x_scales[b][:, tokens],
-                                rhs=w_codes[s][:, columns].bitcast(FP8X4),
-                                rhs_scale=w_scales[s][:, columns],
-                                start=start,
-                                stop=stop,
-                            )
+                straight_left = terms.tile([P, 2, HEADS, PAIRS], F32, name="straight_left")
+                straight_right = terms.tile([P, 2, HEADS, PAIRS], F32, name="straight_right")
+                crossed_left = terms.tile([P, 2, HEADS, PAIRS, 2], F32, name="crossed_left")
+                crossed_right = terms.tile([P, 2, HEADS, PAIRS, 2], F32, name="crossed_right")
 
-                    def copy_raw(i):
-                        nc.scalar.copy(
-                            out=raw[:, :, i, :, :],
-                            in_=product[i - first][:].rearrange("p a (h m) -> p h m a", h=HEADS),
-                        )
+                pair_sum = sum_pairs(s, b, 0)
+                own = [project(s, b, 0), project(s, b, 1)]
+                for i in (0, 1):
+                    copy_raw(own[i], raw_pairs, i)
+                multiply_straight(pair_sum, 0, straight_left)
+                for i in (0, 1):
+                    multiply_crossed(own[i], i, crossed_left[:, i, :, :, :])
 
-                    straight = terms.tile([P, 2, HEADS, PAIRS], F32, name="straight")
-                    crossed = terms.tile([P, 2, HEADS, PAIRS, 2], F32, name="crossed")
+                values = None
+                if s == 0:
+                    tiles, places, values = next_operand(b)
+                    for t in range(2):
+                        bank = banks.tile([P, 2, 2, P], F32, name="bank")
+                        turn(tiles[t], bank)
+                        spread(nc.scalar.copy, bank, places[t])
 
-                    def multiply_crossed(i):
-                        nc.vector.tensor_tensor(
-                            out=crossed[:, i - first, :, :, :],
-                            in0=product[i - first][:, ::-1, :].rearrange("p a (h m) -> p h m a", h=HEADS),
-                            in1=cross[:, i, :, :].unsqueeze(1).to_broadcast([P, HEADS, PAIRS, 2]),
-                            op=ALU.mult,
-                        )
-
-                    copy_raw(first)
-                    nc.vector.tensor_tensor(
-                        out=straight[:],
-                        in0=pair_sum[:].rearrange("p i (h m) -> p i h m", h=HEADS),
-                        in1=cosine[:, first : first + 2, :].unsqueeze(2).to_broadcast([P, 2, HEADS, PAIRS]),
-                        op=ALU.mult,
-                    )
-                    multiply_crossed(first)
-                    copy_raw(first + 1)
-                    multiply_crossed(first + 1)
-                    for i in (first, first + 1):
-                        adder = nc.vector if i == first else nc.gpsimd
-                        adder.tensor_tensor(
-                            out=rotated[:, :, i, :].rearrange("p h (m a) -> p h m a", a=2),
-                            in0=straight[:, i - first, :, :].unsqueeze(3).to_broadcast([P, HEADS, PAIRS, 2]),
-                            in1=crossed[:, i - first, :, :, :],
-                            op=ALU.add,
-                        )
-                    if first == 0 and grouped is not None:
-                        quantise(*grouped)
-                nc.sync.dma_start(
-                    out=raw_outs[s][b].rearrange("h (p i) f -> p h (i f)", i=SUB),
-                    in_=raw[:].rearrange("p h i m a -> p h (i m a)"),
-                )
-                nc.sync.dma_start(
-                    out=rotated_outs[s][b].rearrange("h (p i) f -> p h (i f)", i=SUB),
-                    in_=rotated[:].rearrange("p h i f -> p h (i f)"),
-                )
+                pair_sum = sum_pairs(s, b, 2)
+                own = [project(s, b, 2), project(s, b, 3)]
+                for i in (2, 3):
+                    copy_raw(own[i - 2], raw_pairs, i)
+                multiply_straight(pair_sum, 2, straight_right)
+                if late is not None:
+                    add(nc.vector, late[2], late[3], late[4], 0)
+                    store(rotated_outs[late[0]], late[1], late[4])
+                last = s == 1 and b == BATCH - 1
+                if last:
+                    add(nc.vector, straight_left, crossed_left, rotated, 0)
+                if values is not None:
+                    quantise(*values)
+                for i in (2, 3):
+                    multiply_crossed(own[i - 2], i, crossed_right[:, i - 2, :, :, :])
+                add(nc.vector if last else nc.gpsimd, straight_right, crossed_right, rotated, 2)
+                store(raw_outs[s], b, raw)
+                late = (s, b, straight_left, crossed_left, rotated)
+        store(rotated_outs[1], BATCH - 1, rotated)

@@ -212,18 +212,24 @@ def tile_ropeattnlayer_pa_t_kernel(tc, x, w_qk, out_0, out_1, out_2, out_3):
                 slice(pair * 2 * P, (pair + 1) * 2 * P),
             )
 
-        def next_operand(b):
-            if b + 1 < BATCH:
+        def group(b):
+            if b < BATCH:
                 x_grouped = x_stage()
-                tiles = [x_tiles(b + 1, pair) for pair in range(2)]
+                tiles = [x_tiles(b, pair) for pair in range(2)]
                 places = [x_grouped[:, 2 * pair : 2 * pair + 2, :] for pair in range(2)]
                 values = x_grouped[:].rearrange("p i v -> p (i v)")
-                return tiles, places, (values, x_codes[b + 1], x_scales[b + 1], slice(0, POSITIONS))
-            w_grouped = w_stage()
-            tiles = [w_tiles(1, g) for g in range(2)]
-            places = [w_grouped[:, :, g, :] for g in range(2)]
-            values = w_grouped[:].rearrange("p a g v -> p (a g v)")
-            return tiles, places, (values, w_codes[1], w_scales[1], slice(0, CHANNELS))
+                arguments = (values, x_codes[b], x_scales[b], slice(0, POSITIONS))
+            else:
+                w_grouped = w_stage()
+                tiles = [w_tiles(1, g) for g in range(2)]
+                places = [w_grouped[:, :, g, :] for g in range(2)]
+                values = w_grouped[:].rearrange("p a g v -> p (a g v)")
+                arguments = (values, w_codes[1], w_scales[1], slice(0, CHANNELS))
+            for t in range(2):
+                bank = banks.tile([P, 2, 2, P], F32, name="bank")
+                turn(tiles[t], bank)
+                spread(nc.scalar.copy, bank, places[t])
+            return arguments
 
         def multiply(s, b, i, columns, out, start, stop):
             tokens = slice(i * P, (i + 1) * P)
@@ -306,13 +312,11 @@ def tile_ropeattnlayer_pa_t_kernel(tc, x, w_qk, out_0, out_1, out_2, out_3):
                 for i in (0, 1):
                     multiply_crossed(own[i], i, crossed_left[:, i, :, :, :])
 
-                values = None
-                if s == 0:
-                    tiles, places, values = next_operand(b)
-                    for t in range(2):
-                        bank = banks.tile([P, 2, 2, P], F32, name="bank")
-                        turn(tiles[t], bank)
-                        spread(nc.scalar.copy, bank, places[t])
+                if s == 0 and b == 0:
+                    quantise(*group(1))
+                arguments = None
+                if s == 0 and b + 2 <= BATCH:
+                    arguments = group(b + 2)
 
                 pair_sum = sum_pairs(s, b, 2)
                 own = [project(s, b, 2), project(s, b, 3)]
@@ -325,8 +329,8 @@ def tile_ropeattnlayer_pa_t_kernel(tc, x, w_qk, out_0, out_1, out_2, out_3):
                 last = s == 1 and b == BATCH - 1
                 if last:
                     add(nc.vector, straight_left, crossed_left, rotated, 0)
-                if values is not None:
-                    quantise(*values)
+                if arguments is not None:
+                    quantise(*arguments)
                 for i in (2, 3):
                     multiply_crossed(own[i - 2], i, crossed_right[:, i - 2, :, :, :])
                 add(nc.vector if last else nc.gpsimd, straight_right, crossed_right, rotated, 2)

@@ -88,12 +88,15 @@ def rotation_tables(nc, pool, part, size, plus_half_pi, minus_half_pi):
     nc.scalar.activation(
         out=cosine[:], in_=size[:], func=ACT.Sin, bias=plus_half_pi[:], scale=-2.0 * math.pi
     )
-    cross = pool.tile([P, SUB, PAIRS, 2], F32)
+    cross = pool.tile([P, 2, SUB, PAIRS], F32)
     nc.gpsimd.tensor_tensor(
-        out=cross[:, :, :, 0], in0=minus_cosine[:], in1=sine[:], op=ALU.subtract
+        out=cross[:, 0, :, :], in0=minus_cosine[:], in1=sine[:], op=ALU.subtract
     )
-    nc.gpsimd.tensor_tensor(out=cross[:, :, :, 1], in0=minus_cosine[:], in1=sine[:], op=ALU.add)
-    return cosine, cross
+    return cosine, minus_cosine, sine, cross
+
+
+def finish_cross(nc, minus_cosine, sine, cross):
+    nc.vector.tensor_tensor(out=cross[:, 1, :, :], in0=minus_cosine[:], in1=sine[:], op=ALU.add)
 
 
 def tile_ropeattnlayer_pa_t_kernel(tc, x, w_qk, out_0, out_1, out_2, out_3):
@@ -105,7 +108,8 @@ def tile_ropeattnlayer_pa_t_kernel(tc, x, w_qk, out_0, out_1, out_2, out_3):
         keep = ctx.enter_context(tc.tile_pool(name="keep", bufs=1))
         stage = ctx.enter_context(tc.tile_pool(name="stage", bufs=2))
         terms = ctx.enter_context(tc.tile_pool(name="terms", bufs=2))
-        results = ctx.enter_context(tc.tile_pool(name="results", bufs=5))
+        results = ctx.enter_context(tc.tile_pool(name="results", bufs=4))
+        ends = ctx.enter_context(tc.tile_pool(name="ends", bufs=2))
         banks = ctx.enter_context(tc.psum_pool(name="banks", bufs=2))
         products = ctx.enter_context(tc.psum_pool(name="products", bufs=4))
         sums = ctx.enter_context(tc.psum_pool(name="sums", bufs=2))
@@ -135,10 +139,10 @@ def tile_ropeattnlayer_pa_t_kernel(tc, x, w_qk, out_0, out_1, out_2, out_3):
         load_w(0, 1)
         load_x(0, 0, 2)
         load_x(0, 2, 4)
-        for b in range(1, BATCH):
-            load_x(b, 0, SUB)
         load_w(1, 0)
         load_w(1, 1)
+        for b in range(1, BATCH):
+            load_x(b, 0, SUB)
 
         identity = keep.tile([P, P], F32)
         make_identity(nc, identity[:])
@@ -198,19 +202,26 @@ def tile_ropeattnlayer_pa_t_kernel(tc, x, w_qk, out_0, out_1, out_2, out_3):
             x_banks.append(x_bank)
         spread(nc.scalar.copy, w_banks[0], w_grouped[:, :, 0, :])
         spread(nc.vector.tensor_copy, w_banks[1], w_grouped[:, :, 1, :])
-        cosine, cross = rotation_tables(nc, keep, part, size, plus_half_pi, minus_half_pi)
-        for pair in range(2):
-            spread(nc.scalar.copy, x_banks[pair], x_grouped[:, 2 * pair : 2 * pair + 2, :])
-        quantise(
-            w_grouped[:].rearrange("p a g v -> p (a g v)"), w_codes[0], w_scales[0], slice(0, CHANNELS)
+        spread(nc.scalar.copy, x_banks[0], x_grouped[:, 0:2, :])
+        cosine, minus_cosine, sine, cross = rotation_tables(
+            nc, keep, part, size, plus_half_pi, minus_half_pi
         )
-        for pair in range(2):
+        spread(nc.scalar.copy, x_banks[1], x_grouped[:, 2:4, :])
+
+        def quantise_first_x(pair):
             quantise(
                 x_grouped[:, 2 * pair : 2 * pair + 2, :].rearrange("p i v -> p (i v)"),
                 x_codes[0],
                 x_scales[0],
                 slice(pair * 2 * P, (pair + 1) * 2 * P),
             )
+
+        quantise(
+            w_grouped[:].rearrange("p a g v -> p (a g v)"), w_codes[0], w_scales[0], slice(0, CHANNELS)
+        )
+        quantise_first_x(0)
+        finish_cross(nc, minus_cosine, sine, cross)
+        quantise_first_x(1)
 
         def group(b):
             if b < BATCH:
@@ -243,97 +254,133 @@ def tile_ropeattnlayer_pa_t_kernel(tc, x, w_qk, out_0, out_1, out_2, out_3):
                 stop=stop,
             )
 
-        def sum_pairs(s, b, first):
+        def project(s, b, first):
             pair_sum = sums.tile([P, 2, ALL_PAIRS], F32, name="pair_sum")
             for t in range(2):
                 for a in range(2):
                     columns = slice(a * ALL_PAIRS, (a + 1) * ALL_PAIRS)
                     multiply(s, b, first + t, columns, pair_sum[:, t, :], a == 0, a == 1)
-            return pair_sum
+            own = []
+            for t in range(2):
+                product = products.tile([P, 2, ALL_PAIRS], F32, name="own")
+                multiply(
+                    s, b, first + t, slice(0, CHANNELS), product[:].rearrange("p a m -> p (a m)"), True, True
+                )
+                own.append(product)
+            return own, pair_sum
 
-        def project(s, b, i):
-            own = products.tile([P, 2, ALL_PAIRS], F32, name="own")
-            multiply(s, b, i, slice(0, CHANNELS), own[:].rearrange("p a m -> p (a m)"), True, True)
-            return own
-
-        def copy_raw(own, raw_pairs, i):
-            nc.scalar.copy(
-                out=raw_pairs[:, :, i, :, :],
-                in_=own[:].rearrange("p a (h m) -> p h m a", h=HEADS),
-            )
+        def copy_raw(own, raw, place):
+            for t in range(2):
+                nc.scalar.copy(
+                    out=raw[:, :, place + t, :].rearrange("p h (m a) -> p h m a", a=2),
+                    in_=own[t][:].rearrange("p a (h m) -> p h m a", h=HEADS),
+                )
 
         def multiply_straight(pair_sum, first, straight):
             nc.vector.tensor_tensor(
-                out=straight[:],
-                in0=pair_sum[:].rearrange("p i (h m) -> p i h m", h=HEADS),
+                out=straight[:].rearrange("p h t m -> p t h m"),
+                in0=pair_sum[:].rearrange("p t (h m) -> p t h m", h=HEADS),
                 in1=cosine[:, first : first + 2, :].unsqueeze(2).to_broadcast([P, 2, HEADS, PAIRS]),
                 op=ALU.mult,
             )
 
-        def multiply_crossed(own, i, crossed):
-            nc.vector.tensor_tensor(
-                out=crossed,
-                in0=own[:, ::-1, :].rearrange("p a (h m) -> p h m a", h=HEADS),
-                in1=cross[:, i, :, :].unsqueeze(1).to_broadcast([P, HEADS, PAIRS, 2]),
-                op=ALU.mult,
-            )
-
-        def add(engine, straight, crossed, rotated, first):
+        def multiply_crossed(own, first, crossed):
             for t in range(2):
-                engine.tensor_tensor(
-                    out=rotated[:, :, first + t, :].rearrange("p h (m a) -> p h m a", a=2),
-                    in0=straight[:, t, :, :].unsqueeze(3).to_broadcast([P, HEADS, PAIRS, 2]),
-                    in1=crossed[:, t, :, :, :],
-                    op=ALU.add,
+                nc.vector.tensor_tensor(
+                    out=crossed[:, :, t, :, :],
+                    in0=own[t][:, ::-1, :].rearrange("p a (h m) -> p h m a", h=HEADS),
+                    in1=cross[:, :, first + t, :]
+                    .rearrange("p a m -> p m a")
+                    .unsqueeze(1)
+                    .to_broadcast([P, HEADS, PAIRS, 2]),
+                    op=ALU.mult,
                 )
 
-        def store(outs, b, result):
+        def add_both(straight, crossed, rotated, place):
+            nc.vector.tensor_tensor(
+                out=rotated[:, :, place : place + 2, :].rearrange("p h t (m a) -> p h t m a", a=2),
+                in0=straight[:].unsqueeze(4).to_broadcast([P, HEADS, 2, PAIRS, 2]),
+                in1=crossed[:],
+                op=ALU.add,
+            )
+
+        def add_one(engine, straight, crossed, rotated, place, t):
+            engine.tensor_tensor(
+                out=rotated[:, :, place + t, :].rearrange("p h (m a) -> p h m a", a=2),
+                in0=straight[:, :, t, :].unsqueeze(3).to_broadcast([P, HEADS, PAIRS, 2]),
+                in1=crossed[:, :, t, :, :],
+                op=ALU.add,
+            )
+
+        def store(outs, b, result, first, last):
+            out = outs[b].rearrange("h (p i) f -> p h i f", i=SUB)
             nc.sync.dma_start(
-                out=outs[b].rearrange("h (p i) f -> p h (i f)", i=SUB),
+                out=out[:, :, first:last, :].rearrange("p h i f -> p h (i f)"),
                 in_=result[:].rearrange("p h i f -> p h (i f)"),
             )
 
-        late = None
-        for s in range(2):
-            for b in range(BATCH):
-                raw = results.tile([P, HEADS, SUB, HEAD_DIM], F32, name="raw")
-                raw_pairs = raw[:].rearrange("p h i (m a) -> p h i m a", a=2)
-                rotated = results.tile([P, HEADS, SUB, HEAD_DIM], F32, name="rotated")
-                straight_left = terms.tile([P, 2, HEADS, PAIRS], F32, name="straight_left")
-                straight_right = terms.tile([P, 2, HEADS, PAIRS], F32, name="straight_right")
-                crossed_left = terms.tile([P, 2, HEADS, PAIRS, 2], F32, name="crossed_left")
-                crossed_right = terms.tile([P, 2, HEADS, PAIRS, 2], F32, name="crossed_right")
+        for b in range(BATCH):
+            for s in range(2):
+                first = b == 0 and s == 0
+                halves = b == 0 or (b == BATCH - 1 and s == 1)
+                last = b == BATCH - 1 and s == 1
+                third_add = s == 1 and b % 2 == 0 and b > 0
+                raws = []
+                rotateds = []
+                if halves:
+                    for half in ("left", "right"):
+                        raws.append((ends.tile([P, HEADS, 2, HEAD_DIM], F32, name="raw_" + half), 0))
+                        rotateds.append((ends.tile([P, HEADS, 2, HEAD_DIM], F32, name="rotated_" + half), 0))
+                else:
+                    raw = results.tile([P, HEADS, SUB, HEAD_DIM], F32, name="raw")
+                    rotated = results.tile([P, HEADS, SUB, HEAD_DIM], F32, name="rotated")
+                    for place in (0, 2):
+                        raws.append((raw, place))
+                        rotateds.append((rotated, place))
+                straight_left = terms.tile([P, HEADS, 2, PAIRS], F32, name="straight_left")
+                straight_right = terms.tile([P, HEADS, 2, PAIRS], F32, name="straight_right")
+                crossed_left = terms.tile([P, HEADS, 2, PAIRS, 2], F32, name="crossed_left")
+                crossed_right = terms.tile([P, HEADS, 2, PAIRS, 2], F32, name="crossed_right")
 
-                pair_sum = sum_pairs(s, b, 0)
-                own = [project(s, b, 0), project(s, b, 1)]
-                for i in (0, 1):
-                    copy_raw(own[i], raw_pairs, i)
+                own, pair_sum = project(s, b, 0)
+                copy_raw(own, *raws[0])
                 multiply_straight(pair_sum, 0, straight_left)
-                for i in (0, 1):
-                    multiply_crossed(own[i], i, crossed_left[:, i, :, :, :])
+                multiply_crossed(own, 0, crossed_left)
 
-                if s == 0 and b == 0:
-                    quantise(*group(1))
+                making = None
+                if first:
+                    making = BATCH
+                elif b == 0:
+                    making = 1
+                elif s == 0 and b + 1 < BATCH:
+                    making = b + 1
                 arguments = None
-                if s == 0 and b + 2 <= BATCH:
-                    arguments = group(b + 2)
-
-                pair_sum = sum_pairs(s, b, 2)
-                own = [project(s, b, 2), project(s, b, 3)]
-                for i in (2, 3):
-                    copy_raw(own[i - 2], raw_pairs, i)
+                if making is not None and not first:
+                    arguments = group(making)
+                own, pair_sum = project(s, b, 2)
+                copy_raw(own, *raws[1])
+                if first:
+                    arguments = group(making)
                 multiply_straight(pair_sum, 2, straight_right)
-                if late is not None:
-                    add(nc.vector, late[2], late[3], late[4], 0)
-                    store(rotated_outs[late[0]], late[1], late[4])
-                last = s == 1 and b == BATCH - 1
-                if last:
-                    add(nc.vector, straight_left, crossed_left, rotated, 0)
+                if third_add:
+                    add_one(nc.vector, straight_left, crossed_left, *rotateds[0], 0)
+                else:
+                    add_both(straight_left, crossed_left, *rotateds[0])
                 if arguments is not None:
                     quantise(*arguments)
-                for i in (2, 3):
-                    multiply_crossed(own[i - 2], i, crossed_right[:, i - 2, :, :, :])
-                add(nc.vector if last else nc.gpsimd, straight_right, crossed_right, rotated, 2)
-                store(raw_outs[s], b, raw)
-                late = (s, b, straight_left, crossed_left, rotated)
-        store(rotated_outs[1], BATCH - 1, rotated)
+                multiply_crossed(own, 2, crossed_right)
+                if last:
+                    add_both(straight_right, crossed_right, *rotateds[1])
+                else:
+                    for t in range(2):
+                        add_one(nc.gpsimd, straight_right, crossed_right, *rotateds[1], t)
+                    if third_add:
+                        add_one(nc.gpsimd, straight_left, crossed_left, *rotateds[0], 1)
+                if halves:
+                    store(raw_outs[s], b, raws[0][0], 0, 2)
+                    store(rotated_outs[s], b, rotateds[0][0], 0, 2)
+                    store(raw_outs[s], b, raws[1][0], 2, SUB)
+                    store(rotated_outs[s], b, rotateds[1][0], 2, SUB)
+                else:
+                    store(raw_outs[s], b, raw, 0, SUB)
+                    store(rotated_outs[s], b, rotated, 0, SUB)

@@ -312,19 +312,35 @@ def tile_ropeattnlayer_pa_t_kernel(tc, x, w_qk, out_0, out_1, out_2, out_3):
                 op=ALU.add,
             )
 
-        def store(outs, b, result, first, last):
+        def add_on_tensor(straight, crossed, rotated, place, t):
+            bank = banks.tile([P, HEADS, PAIRS, 2], F32, name="bank")
+            nc.tensor.matmul(
+                bank[:], lhsT=identity[:], rhs=crossed[:, :, t, :, :], start=True, stop=False
+            )
+            nc.tensor.matmul(
+                bank[:],
+                lhsT=identity[:],
+                rhs=straight[:, :, t, :].unsqueeze(3).to_broadcast([P, HEADS, PAIRS, 2]),
+                start=False,
+                stop=True,
+            )
+            nc.scalar.copy(
+                out=rotated[:, :, place + t, :].rearrange("p h (m a) -> p h m a", a=2), in_=bank[:]
+            )
+
+        def store(queue, outs, b, result, first, last):
             out = outs[b].rearrange("h (p i) f -> p h i f", i=SUB)
-            nc.sync.dma_start(
+            queue.dma_start(
                 out=out[:, :, first:last, :].rearrange("p h i f -> p h (i f)"),
                 in_=result[:].rearrange("p h i f -> p h (i f)"),
             )
 
+        tensor_adds = []
         for b in range(BATCH):
             for s in range(2):
                 first = b == 0 and s == 0
-                halves = b == 0 or (b == BATCH - 1 and s == 1)
                 last = b == BATCH - 1 and s == 1
-                third_add = s == 1 and b % 2 == 0 and b > 0
+                halves = first or last
                 raws = []
                 rotateds = []
                 if halves:
@@ -344,6 +360,10 @@ def tile_ropeattnlayer_pa_t_kernel(tc, x, w_qk, out_0, out_1, out_2, out_3):
 
                 own, pair_sum = project(s, b, 0)
                 copy_raw(own, *raws[0])
+                for straight, crossed, queued_rotated in tensor_adds:
+                    add_on_tensor(straight, crossed, queued_rotated, 0, 1)
+                    store(nc.sync, rotated_outs[0], b, queued_rotated, 0, SUB)
+                tensor_adds = []
                 multiply_straight(pair_sum, 0, straight_left)
                 multiply_crossed(own, 0, crossed_left)
 
@@ -359,11 +379,17 @@ def tile_ropeattnlayer_pa_t_kernel(tc, x, w_qk, out_0, out_1, out_2, out_3):
                     arguments = group(making)
                 own, pair_sum = project(s, b, 2)
                 copy_raw(own, *raws[1])
+                if halves:
+                    for half in range(2):
+                        store(nc.scalar, raw_outs[s], b, raws[half][0], 2 * half, 2 * half + 2)
+                else:
+                    store(nc.scalar, raw_outs[s], b, raw, 0, SUB)
                 if first:
                     arguments = group(making)
                 multiply_straight(pair_sum, 2, straight_right)
-                if third_add:
+                if s == 0 and not first:
                     add_one(nc.vector, straight_left, crossed_left, *rotateds[0], 0)
+                    tensor_adds.append((straight_left, crossed_left, rotated))
                 else:
                     add_both(straight_left, crossed_left, *rotateds[0])
                 if arguments is not None:
@@ -374,13 +400,8 @@ def tile_ropeattnlayer_pa_t_kernel(tc, x, w_qk, out_0, out_1, out_2, out_3):
                 else:
                     for t in range(2):
                         add_one(nc.gpsimd, straight_right, crossed_right, *rotateds[1], t)
-                    if third_add:
-                        add_one(nc.gpsimd, straight_left, crossed_left, *rotateds[0], 1)
                 if halves:
-                    store(raw_outs[s], b, raws[0][0], 0, 2)
-                    store(rotated_outs[s], b, rotateds[0][0], 0, 2)
-                    store(raw_outs[s], b, raws[1][0], 2, SUB)
-                    store(rotated_outs[s], b, rotateds[1][0], 2, SUB)
-                else:
-                    store(raw_outs[s], b, raw, 0, SUB)
-                    store(rotated_outs[s], b, rotated, 0, SUB)
+                    for half in range(2):
+                        store(nc.sync, rotated_outs[s], b, rotateds[half][0], 2 * half, 2 * half + 2)
+                elif s == 1:
+                    store(nc.sync, rotated_outs[s], b, rotated, 0, SUB)

@@ -192,14 +192,25 @@ def tile_ropeattnlayer_pa_t_kernel(tc, x, w_qk, out_0, out_1, out_2, out_3):
         part, size, plus_half_pi, minus_half_pi = reduce_angles(nc, keep)
         w_banks = []
         x_banks = []
+
+        idle_bank = products.tile([P, P], F32, name="own")
+
+        def keep_busy(times):
+            for t in range(times):
+                nc.tensor.matmul(idle_bank[:], lhsT=identity[:], rhs=identity[:], start=True, stop=True)
+
+        keep_busy(3)
         for g in range(2):
             w_bank = banks.tile([P, 2, 2, P], F32, name="bank")
             turn(w_tiles(0, g), w_bank)
+            keep_busy(1)
             w_banks.append(w_bank)
         for pair in range(2):
             x_bank = products.tile([P, 2, 2, P], F32, name="own")
             turn(x_tiles(0, pair), x_bank)
+            keep_busy(1)
             x_banks.append(x_bank)
+        keep_busy(2)
         spread(nc.scalar.copy, w_banks[0], w_grouped[:, :, 0, :])
         spread(nc.vector.tensor_copy, w_banks[1], w_grouped[:, :, 1, :])
         spread(nc.scalar.copy, x_banks[0], x_grouped[:, 0:2, :])
@@ -221,7 +232,6 @@ def tile_ropeattnlayer_pa_t_kernel(tc, x, w_qk, out_0, out_1, out_2, out_3):
         )
         quantise_first_x(0)
         finish_cross(nc, minus_cosine, sine, cross)
-        quantise_first_x(1)
 
         def group(b):
             if b < BATCH:
@@ -365,6 +375,8 @@ def tile_ropeattnlayer_pa_t_kernel(tc, x, w_qk, out_0, out_1, out_2, out_3):
                     store(nc.sync, rotated_outs[0], b, queued_rotated, 0, SUB)
                 tensor_adds = []
                 multiply_straight(pair_sum, 0, straight_left)
+                if first:
+                    quantise_first_x(1)
                 multiply_crossed(own, 0, crossed_left)
 
                 making = None
@@ -375,7 +387,7 @@ def tile_ropeattnlayer_pa_t_kernel(tc, x, w_qk, out_0, out_1, out_2, out_3):
                 elif s == 0 and b + 1 < BATCH:
                     making = b + 1
                 arguments = None
-                if making is not None and not first:
+                if making is not None:
                     arguments = group(making)
                 own, pair_sum = project(s, b, 2)
                 copy_raw(own, *raws[1])
@@ -384,10 +396,11 @@ def tile_ropeattnlayer_pa_t_kernel(tc, x, w_qk, out_0, out_1, out_2, out_3):
                         store(nc.scalar, raw_outs[s], b, raws[half][0], 2 * half, 2 * half + 2)
                 else:
                     store(nc.scalar, raw_outs[s], b, raw, 0, SUB)
-                if first:
-                    arguments = group(making)
                 multiply_straight(pair_sum, 2, straight_right)
-                if s == 0 and not first:
+                if b == 0:
+                    add_one(nc.vector, straight_left, crossed_left, *rotateds[0], 0)
+                    add_on_tensor(straight_left, crossed_left, *rotateds[0], 1)
+                elif s == 0:
                     add_one(nc.vector, straight_left, crossed_left, *rotateds[0], 0)
                     tensor_adds.append((straight_left, crossed_left, rotated))
                 else:

@@ -350,19 +350,21 @@ def tile_ropeattnlayer_pa_t_kernel(tc, x, w_qk, out_0, out_1, out_2, out_3):
             for s in range(2):
                 first = b == 0 and s == 0
                 last = b == BATCH - 1 and s == 1
-                halves = first or last
+                early = b < 2
                 raws = []
-                rotateds = []
-                if halves:
+                if first or last:
                     for half in ("left", "right"):
                         raws.append((ends.tile([P, HEADS, 2, HEAD_DIM], F32, name="raw_" + half), 0))
-                        rotateds.append((ends.tile([P, HEADS, 2, HEAD_DIM], F32, name="rotated_" + half), 0))
                 else:
                     raw = results.tile([P, HEADS, SUB, HEAD_DIM], F32, name="raw")
+                    raws = [(raw, 0), (raw, 2)]
+                rotateds = []
+                if early or last:
+                    for half in ("left", "right"):
+                        rotateds.append((ends.tile([P, HEADS, 2, HEAD_DIM], F32, name="rotated_" + half), 0))
+                else:
                     rotated = results.tile([P, HEADS, SUB, HEAD_DIM], F32, name="rotated")
-                    for place in (0, 2):
-                        raws.append((raw, place))
-                        rotateds.append((rotated, place))
+                    rotateds = [(rotated, 0), (rotated, 2)]
                 straight_left = terms.tile([P, HEADS, 2, PAIRS], F32, name="straight_left")
                 straight_right = terms.tile([P, HEADS, 2, PAIRS], F32, name="straight_right")
                 crossed_left = terms.tile([P, HEADS, 2, PAIRS, 2], F32, name="crossed_left")
@@ -370,9 +372,9 @@ def tile_ropeattnlayer_pa_t_kernel(tc, x, w_qk, out_0, out_1, out_2, out_3):
 
                 own, pair_sum = project(s, b, 0)
                 copy_raw(own, *raws[0])
-                for straight, crossed, queued_rotated in tensor_adds:
-                    add_on_tensor(straight, crossed, queued_rotated, 0, 1)
-                    store(nc.sync, rotated_outs[0], b, queued_rotated, 0, SUB)
+                for straight, crossed, queued, stop in tensor_adds:
+                    add_on_tensor(straight, crossed, queued, 0, 1)
+                    store(nc.sync, rotated_outs[0], b, queued, 0, stop)
                 tensor_adds = []
                 multiply_straight(pair_sum, 0, straight_left)
                 if first:
@@ -391,18 +393,18 @@ def tile_ropeattnlayer_pa_t_kernel(tc, x, w_qk, out_0, out_1, out_2, out_3):
                     arguments = group(making)
                 own, pair_sum = project(s, b, 2)
                 copy_raw(own, *raws[1])
-                if halves:
+                if first or last:
                     for half in range(2):
-                        store(nc.scalar, raw_outs[s], b, raws[half][0], 2 * half, 2 * half + 2)
+                        store(nc.sync, raw_outs[s], b, raws[half][0], 2 * half, 2 * half + 2)
                 else:
-                    store(nc.scalar, raw_outs[s], b, raw, 0, SUB)
+                    store(nc.sync, raw_outs[s], b, raw, 0, SUB)
                 multiply_straight(pair_sum, 2, straight_right)
                 if b == 0:
                     add_one(nc.vector, straight_left, crossed_left, *rotateds[0], 0)
                     add_on_tensor(straight_left, crossed_left, *rotateds[0], 1)
                 elif s == 0:
                     add_one(nc.vector, straight_left, crossed_left, *rotateds[0], 0)
-                    tensor_adds.append((straight_left, crossed_left, rotated))
+                    tensor_adds.append((straight_left, crossed_left, rotateds[0][0], 2 if early else SUB))
                 else:
                     add_both(straight_left, crossed_left, *rotateds[0])
                 if arguments is not None:
@@ -413,8 +415,9 @@ def tile_ropeattnlayer_pa_t_kernel(tc, x, w_qk, out_0, out_1, out_2, out_3):
                 else:
                     for t in range(2):
                         add_one(nc.gpsimd, straight_right, crossed_right, *rotateds[1], t)
-                if halves:
-                    for half in range(2):
-                        store(nc.sync, rotated_outs[s], b, rotateds[half][0], 2 * half, 2 * half + 2)
+                if early or last:
+                    if s == 1 or first:
+                        store(nc.sync, rotated_outs[s], b, rotateds[0][0], 0, 2)
+                    store(nc.sync, rotated_outs[s], b, rotateds[1][0], 2, SUB)
                 elif s == 1:
                     store(nc.sync, rotated_outs[s], b, rotated, 0, SUB)

import math
from contextlib import ExitStack

import concourse.mybir as mybir
from concourse.masks import make_identity

F32 = mybir.dt.float32
BF16 = mybir.dt.bfloat16
I32 = mybir.dt.int32
U32 = mybir.dt.uint32
U8 = mybir.dt.uint8
FP8X4 = mybir.dt.float8_e4m3fn_x4
ALU = mybir.AluOpType
ACT = mybir.ActivationFunctionType

P = 128
BATCH, POSITIONS, CHANNELS, HEADS = 8, 512, 512, 4
HEAD_DIM = CHANNELS // HEADS
PAIRS = HEAD_DIM // 2
ALL_PAIRS = HEADS * PAIRS
WORDS = CHANNELS // 2
SUB = POSITIONS // P

FLOPS = 2 * BATCH * POSITIONS * CHANNELS * 2 * CHANNELS

ROUND_MAGIC = 12582912.0


def reduce_angles(nc, pool):
    position_int = pool.tile([P, SUB], I32)
    nc.gpsimd.iota(position_int[:], pattern=[[1, SUB]], base=1, channel_multiplier=SUB)

    one = pool.tile([P, 1], F32)
    nc.vector.memset(one[:], 1.0)
    warm = pool.tile([P, 1], F32)
    nc.scalar.activation(out=warm[:], in_=one[:], func=ACT.Sin)

    ratio = 1000.0 ** (-2.0 / HEAD_DIM)
    frequency = pool.tile([P, PAIRS], F32)
    nc.vector.tensor_scalar_mul(out=frequency[:, 0:1], in0=one[:], scalar1=ratio / (2.0 * math.pi))
    half = 1
    while half < PAIRS:
        nc.vector.tensor_scalar_mul(
            out=frequency[:, half : 2 * half], in0=frequency[:, 0:half], scalar1=ratio**half
        )
        half *= 2
    plus_half_pi = pool.tile([P, 1], F32)
    nc.vector.tensor_scalar_mul(out=plus_half_pi[:], in0=one[:], scalar1=0.5 * math.pi)
    minus_half_pi = pool.tile([P, 1], F32)
    nc.vector.tensor_scalar_mul(out=minus_half_pi[:], in0=one[:], scalar1=-0.5 * math.pi)
    position = pool.tile([P, SUB], F32)
    nc.vector.tensor_copy(out=position[:], in_=position_int[:])

    turns = pool.tile([P, SUB, PAIRS], F32)
    nc.vector.tensor_tensor(
        out=turns[:],
        in0=position[:].unsqueeze(2).to_broadcast([P, SUB, PAIRS]),
        in1=frequency[:].unsqueeze(1).to_broadcast([P, SUB, PAIRS]),
        op=ALU.mult,
    )
    whole = pool.tile([P, SUB, PAIRS], F32)
    nc.vector.tensor_scalar(
        out=whole[:],
        in0=turns[:],
        scalar1=ROUND_MAGIC,
        scalar2=ROUND_MAGIC,
        op0=ALU.add,
        op1=ALU.subtract,
    )
    part = pool.tile([P, SUB, PAIRS], F32)
    nc.vector.tensor_tensor(out=part[:], in0=turns[:], in1=whole[:], op=ALU.subtract)
    size = pool.tile([P, SUB, PAIRS], F32)
    nc.vector.scalar_tensor_tensor(
        out=size[:], in0=part[:], scalar=-1.0, in1=part[:], op0=ALU.mult, op1=ALU.max
    )

    return part, size, plus_half_pi, minus_half_pi


def rotation_tables(nc, pool, part, size, plus_half_pi, minus_half_pi):
    sine = pool.tile([P, SUB, PAIRS], F32)
    nc.scalar.activation(out=sine[:], in_=part[:], func=ACT.Sin, scale=2.0 * math.pi)
    minus_cosine = pool.tile([P, SUB, PAIRS], F32)
    nc.scalar.activation(
        out=minus_cosine[:], in_=size[:], func=ACT.Sin, bias=minus_half_pi[:], scale=2.0 * math.pi
    )
    cosine = pool.tile([P, SUB, PAIRS], F32)
    nc.scalar.activation(
        out=cosine[:], in_=size[:], func=ACT.Sin, bias=plus_half_pi[:], scale=-2.0 * math.pi
    )
    cross = pool.tile([P, 2, SUB, PAIRS], F32)
    nc.gpsimd.tensor_tensor(
        out=cross[:, 0, :, :], in0=minus_cosine[:], in1=sine[:], op=ALU.subtract
    )
    return cosine, minus_cosine, sine, cross


def finish_cross(nc, minus_cosine, sine, cross):
    nc.vector.tensor_tensor(out=cross[:, 1, :, :], in0=minus_cosine[:], in1=sine[:], op=ALU.add)


def tile_ropeattnlayer_pa_t_kernel(tc, x, w_qk, out_0, out_1, out_2, out_3):
    nc = tc.nc
    raw_outs = (out_0, out_1)
    rotated_outs = (out_2, out_3)

    with ExitStack() as ctx:
        keep = ctx.enter_context(tc.tile_pool(name="keep", bufs=1))
        stage = ctx.enter_context(tc.tile_pool(name="stage", bufs=2))
        terms = ctx.enter_context(tc.tile_pool(name="terms", bufs=2))
        results = ctx.enter_context(tc.tile_pool(name="results", bufs=4))
        ends = ctx.enter_context(tc.tile_pool(name="ends", bufs=2))
        banks = ctx.enter_context(tc.psum_pool(name="banks", bufs=2))
        products = ctx.enter_context(tc.psum_pool(name="products", bufs=4))
        sums = ctx.enter_context(tc.psum_pool(name="sums", bufs=2))
        ctx.enter_context(tc.manual_schedule())

        x_rows = []
        for b in range(BATCH):
            x_rows.append(keep.tile([P, SUB, CHANNELS], BF16, name="x_rows_%d" % b))
        w_rows = []
        for s in range(2):
            w_rows.append(keep.tile([P, 2, 2, CHANNELS], BF16, name="w_rows_%d" % s))

        def load_x(b, first, last):
            nc.sync.dma_start(
                out=x_rows[b][:, first:last, :],
                in_=x[b].rearrange("(p i) c -> p i c", i=SUB)[:, first:last, :],
            )

        def load_w(s, g):
            start = s * CHANNELS + g * 2 * P
            nc.sync.dma_start(
                out=w_rows[s][:, g, :, :],
                in_=w_qk[start : start + 2 * P, :].rearrange("(p a) c -> p a c", a=2),
            )

        load_w(0, 0)
        load_w(0, 1)
        load_x(0, 0, 2)
        load_x(0, 2, 4)
        load_w(1, 0)
        load_w(1, 1)
        for b in range(1, BATCH):
            load_x(b, 0, SUB)

        identity = keep.tile([P, P], F32)
        make_identity(nc, identity[:])

        def turn(tiles, bank):
            for t in range(2):
                words = tiles[t].bitcast(F32)
                for u in range(2):
                    nc.tensor.transpose(bank[:, t, u, :], words[:, u:WORDS:2], identity[:])

        def spread(copy, bank, grouped):
            copy(
                out=grouped.bitcast(F32).rearrange("p t (r u) -> p t r u", u=2),
                in_=bank[:].rearrange("p t u r -> p t r u"),
            )

        def quantise(grouped, codes, scales, columns):
            nc.vector.quantize_mx(
                out=codes[:, columns].bitcast(FP8X4), scales=scales[:, columns], in_=grouped
            )

        x_codes = []
        x_scales = []
        for b in range(BATCH):
            x_codes.append(keep.tile([P, POSITIONS], U32, name="x_codes_%d" % b, align_bytes=64))
            x_scales.append(keep.tile([P, POSITIONS], U8, name="x_scales_%d" % b, align_bytes=64))
        w_codes = []
        w_scales = []
        for s in range(2):
            w_codes.append(keep.tile([P, CHANNELS], U32, name="w_codes_%d" % s, align_bytes=64))
            w_scales.append(keep.tile([P, CHANNELS], U8, name="w_scales_%d" % s, align_bytes=64))

        def x_tiles(b, pair):
            return [x_rows[b][:, 2 * pair + t, :] for t in range(2)]

        def w_tiles(s, g):
            return [w_rows[s][:, g, a, :] for a in range(2)]

        def x_stage():
            return stage.tile([P, SUB, 4 * P], BF16, name="x_grouped", align_bytes=64)

        def w_stage():
            return stage.tile([P, 2, 2, 4 * P], BF16, name="w_grouped", align_bytes=64)

        w_grouped = w_stage()
        x_grouped = x_stage()
        part, size, plus_half_pi, minus_half_pi = reduce_angles(nc, keep)
        w_banks = []
        x_banks = []

        idle_bank = products.tile([P, P], F32, name="own")

        def keep_busy(times):
            for t in range(times):
                nc.tensor.matmul(idle_bank[:], lhsT=identity[:], rhs=identity[:], start=True, stop=True)

        keep_busy(3)
        for g in range(2):
            w_bank = banks.tile([P, 2, 2, P], F32, name="bank")
            turn(w_tiles(0, g), w_bank)
            keep_busy(1)
            w_banks.append(w_bank)
        for pair in range(2):
            x_bank = products.tile([P, 2, 2, P], F32, name="own")
            turn(x_tiles(0, pair), x_bank)
            keep_busy(1)
            x_banks.append(x_bank)
        keep_busy(2)
        spread(nc.scalar.copy, w_banks[0], w_grouped[:, :, 0, :])
        spread(nc.vector.tensor_copy, w_banks[1], w_grouped[:, :, 1, :])
        spread(nc.scalar.copy, x_banks[0], x_grouped[:, 0:2, :])
        cosine, minus_cosine, sine, cross = rotation_tables(
            nc, keep, part, size, plus_half_pi, minus_half_pi
        )
        spread(nc.scalar.copy, x_banks[1], x_grouped[:, 2:4, :])

        def quantise_first_x(pair):
            quantise(
                x_grouped[:, 2 * pair : 2 * pair + 2, :].rearrange("p i v -> p (i v)"),
                x_codes[0],
                x_scales[0],
                slice(pair * 2 * P, (pair + 1) * 2 * P),
            )

        quantise(
            w_grouped[:].rearrange("p a g v -> p (a g v)"), w_codes[0], w_scales[0], slice(0, CHANNELS)
        )
        quantise_first_x(0)
        finish_cross(nc, minus_cosine, sine, cross)

        def group(b):
            if b < BATCH:
                x_grouped = x_stage()
                tiles = [x_tiles(b, pair) for pair in range(2)]
                places = [x_grouped[:, 2 * pair : 2 * pair + 2, :] for pair in range(2)]
                values = x_grouped[:].rearrange("p i v -> p (i v)")
                arguments = (values, x_codes[b], x_scales[b], slice(0, POSITIONS))
            else:
                w_grouped = w_stage()
                tiles = [w_tiles(1, g) for g in range(2)]
                places = [w_grouped[:, :, g, :] for g in range(2)]
                values = w_grouped[:].rearrange("p a g v -> p (a g v)")
                arguments = (values, w_codes[1], w_scales[1], slice(0, CHANNELS))
            for t in range(2):
                bank = banks.tile([P, 2, 2, P], F32, name="bank")
                turn(tiles[t], bank)
                spread(nc.scalar.copy, bank, places[t])
            return arguments

        def multiply(s, b, i, columns, out, start, stop):
            tokens = slice(i * P, (i + 1) * P)
            nc.tensor.matmul_mx(
                out=out,
                lhsT=x_codes[b][:, tokens].bitcast(FP8X4),
                lhsT_scale=x_scales[b][:, tokens],
                rhs=w_codes[s][:, columns].bitcast(FP8X4),
                rhs_scale=w_scales[s][:, columns],
                start=start,
                stop=stop,
            )

        def project(s, b, first):
            pair_sum = sums.tile([P, 2, ALL_PAIRS], F32, name="pair_sum")
            for t in range(2):
                for a in range(2):
                    columns = slice(a * ALL_PAIRS, (a + 1) * ALL_PAIRS)
                    multiply(s, b, first + t, columns, pair_sum[:, t, :], a == 0, a == 1)
            own = []
            for t in range(2):
                product = products.tile([P, 2, ALL_PAIRS], F32, name="own")
                multiply(
                    s, b, first + t, slice(0, CHANNELS), product[:].rearrange("p a m -> p (a m)"), True, True
                )
                own.append(product)
            return own, pair_sum

        def copy_raw(own, raw, place):
            for t in range(2):
                nc.scalar.copy(
                    out=raw[:, :, place + t, :].rearrange("p h (m a) -> p h m a", a=2),
                    in_=own[t][:].rearrange("p a (h m) -> p h m a", h=HEADS),
                )

        def multiply_straight(pair_sum, first, straight):
            nc.vector.tensor_tensor(
                out=straight[:].rearrange("p h t m -> p t h m"),
                in0=pair_sum[:].rearrange("p t (h m) -> p t h m", h=HEADS),
                in1=cosine[:, first : first + 2, :].unsqueeze(2).to_broadcast([P, 2, HEADS, PAIRS]),
                op=ALU.mult,
            )

        def multiply_crossed(own, first, crossed):
            for t in range(2):
                nc.vector.tensor_tensor(
                    out=crossed[:, :, t, :, :],
                    in0=own[t][:, ::-1, :].rearrange("p a (h m) -> p h m a", h=HEADS),
                    in1=cross[:, :, first + t, :]
                    .rearrange("p a m -> p m a")
                    .unsqueeze(1)
                    .to_broadcast([P, HEADS, PAIRS, 2]),
                    op=ALU.mult,
                )

        def add_both(straight, crossed, rotated, place):
            nc.vector.tensor_tensor(
                out=rotated[:, :, place : place + 2, :].rearrange("p h t (m a) -> p h t m a", a=2),
                in0=straight[:].unsqueeze(4).to_broadcast([P, HEADS, 2, PAIRS, 2]),
                in1=crossed[:],
                op=ALU.add,
            )

        def add_one(engine, straight, crossed, rotated, place, t):
            engine.tensor_tensor(
                out=rotated[:, :, place + t, :].rearrange("p h (m a) -> p h m a", a=2),
                in0=straight[:, :, t, :].unsqueeze(3).to_broadcast([P, HEADS, PAIRS, 2]),
                in1=crossed[:, :, t, :, :],
                op=ALU.add,
            )

        def add_on_tensor(straight, crossed, rotated, place, t):
            bank = banks.tile([P, HEADS, PAIRS, 2], F32, name="bank")
            nc.tensor.matmul(
                bank[:], lhsT=identity[:], rhs=crossed[:, :, t, :, :], start=True, stop=False
            )
            nc.tensor.matmul(
                bank[:],
                lhsT=identity[:],
                rhs=straight[:, :, t, :].unsqueeze(3).to_broadcast([P, HEADS, PAIRS, 2]),
                start=False,
                stop=True,
            )
            nc.scalar.copy(
                out=rotated[:, :, place + t, :].rearrange("p h (m a) -> p h m a", a=2), in_=bank[:]
            )

        def store(queue, outs, b, result, first, last):
            out = outs[b].rearrange("h (p i) f -> p h i f", i=SUB)
            queue.dma_start(
                out=out[:, :, first:last, :].rearrange("p h i f -> p h (i f)"),
                in_=result[:].rearrange("p h i f -> p h (i f)"),
            )

        tensor_adds = []
        for b in range(BATCH):
            for s in range(2):
                first = b == 0 and s == 0
                last = b == BATCH - 1 and s == 1
                early = b < 2
                raws = []
                if first or last:
                    for half in ("left", "right"):
                        raws.append((ends.tile([P, HEADS, 2, HEAD_DIM], F32, name="raw_" + half), 0))
                else:
                    raw = results.tile([P, HEADS, SUB, HEAD_DIM], F32, name="raw")
                    raws = [(raw, 0), (raw, 2)]
                rotateds = []
                if early or last:
                    for half in ("left", "right"):
                        rotateds.append((ends.tile([P, HEADS, 2, HEAD_DIM], F32, name="rotated_" + half), 0))
                else:
                    rotated = results.tile([P, HEADS, SUB, HEAD_DIM], F32, name="rotated")
                    rotateds = [(rotated, 0), (rotated, 2)]
                straight_left = terms.tile([P, HEADS, 2, PAIRS], F32, name="straight_left")
                straight_right = terms.tile([P, HEADS, 2, PAIRS], F32, name="straight_right")
                crossed_left = terms.tile([P, HEADS, 2, PAIRS, 2], F32, name="crossed_left")
                crossed_right = terms.tile([P, HEADS, 2, PAIRS, 2], F32, name="crossed_right")

                own, pair_sum = project(s, b, 0)
                copy_raw(own, *raws[0])
                for straight, crossed, queued, stop in tensor_adds:
                    add_on_tensor(straight, crossed, queued, 0, 1)
                    store(nc.sync, rotated_outs[0], b, queued, 0, stop)
                tensor_adds = []
                multiply_straight(pair_sum, 0, straight_left)
                if first:
                    quantise_first_x(1)
                multiply_crossed(own, 0, crossed_left)

                making = None
                if first:
                    making = BATCH
                elif b == 0:
                    making = 1
                elif s == 0 and b + 1 < BATCH:
                    making = b + 1
                arguments = None
                if making is not None:
                    arguments = group(making)
                own, pair_sum = project(s, b, 2)
                copy_raw(own, *raws[1])
                if first or last:
                    for half in range(2):
                        store(nc.sync, raw_outs[s], b, raws[half][0], 2 * half, 2 * half + 2)
                else:
                    store(nc.sync, raw_outs[s], b, raw, 0, SUB)
                multiply_straight(pair_sum, 2, straight_right)
                if b == 0:
                    add_one(nc.vector, straight_left, crossed_left, *rotateds[0], 0)
                    add_on_tensor(straight_left, crossed_left, *rotateds[0], 1)
                elif s == 0:
                    add_one(nc.vector, straight_left, crossed_left, *rotateds[0], 0)
                    tensor_adds.append((straight_left, crossed_left, rotateds[0][0], 2 if early else SUB))
                else:
                    add_both(straight_left, crossed_left, *rotateds[0])
                if arguments is not None:
                    quantise(*arguments)
                multiply_crossed(own, 2, crossed_right)
                if last:
                    add_both(straight_right, crossed_right, *rotateds[1])
                else:
                    for t in range(2):
                        add_one(nc.gpsimd, straight_right, crossed_right, *rotateds[1], t)
                if early or last:
                    if s == 1 or first:
                        store(nc.sync, rotated_outs[s], b, rotateds[0][0], 0, 2)
                    store(nc.sync, rotated_outs[s], b, rotateds[1][0], 2, SUB)
                elif s == 1:
                    store(nc.sync, rotated_outs[s], b, rotated, 0, SUB)
